import numpy as np
import ml_dtypes


def mxq(x, axis, fmt="e4m3"):
    dtype, down = {"e4m3": (ml_dtypes.float8_e4m3fn, 7), "e5m2": (ml_dtypes.float8_e5m2, 14)}[fmt]
    v = np.moveaxis(np.asarray(x, np.float32).astype(ml_dtypes.bfloat16).astype(np.float64), axis, -1)
    blocks = v.reshape(v.shape[:-1] + (-1, 32))
    amax = np.abs(blocks).max(-1, keepdims=True)
    byte = np.maximum(np.where(amax > 0, np.frexp(amax)[1] - 1 + 127, 0) - down, 1)
    scale = np.exp2(byte - 127.0)
    codes = (blocks / scale).astype(np.float32).astype(dtype).astype(np.float64)
    return np.moveaxis((codes * scale).reshape(v.shape), -1, axis)


WIDE = False


def mx_kscale(k):
    if not WIDE:
        return np.ones(k)
    levels = np.array([10, -10, 5, -5, 0])
    a = np.random.permutation(np.resize(levels, k // 512 * 4)).reshape(k // 512, 4)
    idx = np.arange(k)
    return np.exp2(a[idx // 512, idx % 128 // 32])


BF16 = ml_dtypes.bfloat16


def bf(x):
    return np.asarray(x, np.float32).astype(BF16)


def f64(x):
    return np.asarray(x).astype(np.float64)


E2M1 = np.array([0.0, 0.5, 1.0, 1.5, 2.0, 3.0, 4.0, 6.0, -0.0, -0.5, -1.0, -1.5, -2.0, -3.0, -4.0, -6.0])


def pack_weight(w, fmt):
    k, n = w.shape
    w = f64(bf(w)).reshape(k // 32, 32, n)
    amax = np.abs(w).max(1)
    if fmt == "e4m3":
        byte = np.frexp(amax)[1] - 1 + 127 - 7
    else:
        mant, ex = np.frexp(amax / 6.0)
        byte = np.where(mant > 0.5, ex, ex - 1) + 127
    byte = np.clip(np.where(amax > 0, byte, 1), 1, 254)
    scaled = (w * np.exp2(127.0 - byte)[:, None, :]).reshape(k, n).astype(np.float32)
    by_word = np.ascontiguousarray(scaled.reshape(k // 512, 128, 4, n).transpose(0, 1, 3, 2))
    if fmt == "e4m3":
        words = by_word.astype(ml_dtypes.float8_e4m3fn).view(np.uint8)
    else:
        c = by_word.astype(ml_dtypes.float4_e2m1fn).view(np.uint8) & 0xF
        words = c[..., 0::2] | (c[..., 1::2] << 4)
    return np.ascontiguousarray(words), np.ascontiguousarray(byte.astype(np.uint8).reshape(k // 512, 16, n))


def unpack_weight(words, scales, fmt):
    g, p, n, _ = words.shape
    if fmt == "e4m3":
        vals = np.ascontiguousarray(words).view(ml_dtypes.float8_e4m3fn).astype(np.float64)
    else:
        nib = np.empty((g, p, n, 4), np.uint8)
        nib[..., 0::2] = words & 0xF
        nib[..., 1::2] = words >> 4
        vals = E2M1[nib]
    vals = vals * np.repeat(np.exp2(scales.astype(np.float64) - 127.0), 8, axis=1)[..., None]
    return vals.transpose(0, 1, 3, 2).reshape(g * 512, n)


B, T, V, C, K, R = 4, 8, 32, 512, 1024, 256
FMT = "e4m3"


def setup_inputs():
    n = np.random.standard_normal
    s = mx_kscale(C)
    x = 0.7 * n((B, 1, V, C)) + 0.7 * n((B, T, V, C))
    A = bf(np.eye(V) + 0.1 * n((K, V, V)))
    lam = bf(0.25 + 0.1 * np.random.random(1))
    phi_w_words, phi_w_scales = pack_weight(n((C, K)) / np.sqrt(C) / s[:, None], FMT)
    phi_b = bf(0.3 * n(K))
    theta_w_words, theta_w_scales = pack_weight(n((C, K)) / np.sqrt(C) / s[:, None], FMT)
    theta_b = bf(0.3 * n(K))
    kappa_w_words, kappa_w_scales = pack_weight(n((K, K)) / np.sqrt(K), FMT)
    kappa_b = bf(0.3 * n(K))
    return {
        "x": bf(x * s),
        "A": A,
        "lam": lam,
        "phi_w_words": phi_w_words,
        "phi_w_scales": phi_w_scales,
        "phi_b": phi_b,
        "theta_w_words": theta_w_words,
        "theta_w_scales": theta_w_scales,
        "theta_b": theta_b,
        "kappa_w_words": kappa_w_words,
        "kappa_w_scales": kappa_w_scales,
        "kappa_b": kappa_b,
    }


def reference(x, A, lam, phi_w_words, phi_w_scales, phi_b, theta_w_words, theta_w_scales, theta_b, kappa_w_words, kappa_w_scales, kappa_b):
    xq = mxq(f64(x), 3, "e4m3")
    phi_x = ((xq @ unpack_weight(phi_w_words, phi_w_scales, FMT)) + f64(phi_b)).mean(axis=1)
    theta_x = ((xq @ unpack_weight(theta_w_words, theta_w_scales, FMT)) + f64(theta_b)).mean(axis=1)
    F_ij = np.tanh(phi_x[:, :, None, :] - theta_x[:, None, :, :])
    A_hat = np.transpose((mxq(F_ij, 3, "e4m3") @ unpack_weight(kappa_w_words, kappa_w_scales, FMT)) + f64(kappa_b), (0, 3, 1, 2))
    return f64(A)[None] + f64(lam) * A_hat

@@ -1,0 +1,242 @@
+from contextlib import ExitStack
+
+import concourse.masks as masks
+import concourse.mybir as mybir
+
+F32 = mybir.dt.float32
+BF16 = mybir.dt.bfloat16
+I32 = mybir.dt.int32
+U32 = mybir.dt.uint32
+U8 = mybir.dt.uint8
+FP8X4 = mybir.dt.float8_e4m3fn_x4
+ALU = mybir.AluOpType
+ACT = mybir.ActivationFunctionType
+
+P = 128
+PACK = 4
+K_PASS = P * PACK
+B, T, V, C, K = 4, 8, 32, 512, 1024
+GROUPS = K // K_PASS
+N_TILES = K // P
+ROWS = B * V
+U_CHUNK = 16
+CHUNK = U_CHUNK * V
+CHUNKS = B * V // U_CHUNK
+U_VECTOR = 6
+
+PHI_ROW, THETA_ROW, KAPPA_ROW = 0, 4, 8
+
+FLOPS = 2 * (B * T * V) * C * (2 * K) + 2 * (B * V * V) * K * K
+
+
+def tile_attgcn_pa_kernel(
+    tc,
+    x,
+    A,
+    lam,
+    phi_w_words,
+    phi_w_scales,
+    phi_b,
+    theta_w_words,
+    theta_w_scales,
+    theta_b,
+    kappa_w_words,
+    kappa_w_scales,
+    kappa_b,
+    out,
+):
+    nc = tc.nc
+    with ExitStack() as ctx:
+        keep = ctx.enter_context(tc.tile_pool(name="keep", bufs=1))
+        diff_pool = ctx.enter_context(tc.tile_pool(name="diff_pool", bufs=3))
+        f_pool = ctx.enter_context(tc.tile_pool(name="f_pool", bufs=3))
+        code_pool = ctx.enter_context(tc.tile_pool(name="code_pool", bufs=3))
+        out_pool = ctx.enter_context(tc.tile_pool(name="out_pool", bufs=6))
+        th_banks = ctx.enter_context(tc.psum_pool(name="th_banks", bufs=1))
+        banks = ctx.enter_context(tc.psum_pool(name="banks", bufs=6))
+
+        planes = keep.tile([P, K], U8, align_bytes=64)
+        nc.vector.memset(planes[:].bitcast(I32), 0)
+
+        x_sb = keep.tile([P, B * T * V // P, C], BF16)
+        x_rows = x.rearrange("b t v c -> (b t v) c").rearrange("(r p) c -> p r c", p=P)
+        for half in range(2):
+            nc.sync.dma_start(out=x_sb[:, 4 * half : 4 * half + 4, :], in_=x_rows[:, 4 * half : 4 * half + 4, :])
+
+        def load_scale_rows(first_row, scales):
+            groups = scales.shape[0]
+            for quad in range(4):
+                first = 32 * quad + first_row
+                nc.sync.dma_start(
+                    out=planes[first : first + 4 * groups, :].bitcast(I32),
+                    in_=scales[:, 4 * quad : 4 * quad + 4, :].bitcast(I32),
+                )
+
+        def load_words(words_sb, words):
+            nc.sync.dma_start(out=words_sb.bitcast(I32), in_=words.rearrange("p n t -> p (n t)").bitcast(I32))
+
+        load_scale_rows(PHI_ROW, phi_w_scales)
+        load_scale_rows(THETA_ROW, theta_w_scales)
+        phi_words = keep.tile([P, K], U32, align_bytes=64)
+        theta_words = keep.tile([P, K], U32, align_bytes=64)
+        load_words(phi_words[:], phi_w_words[0])
+        load_words(theta_words[:], theta_w_words[0])
+        load_scale_rows(KAPPA_ROW, kappa_w_scales)
+        kappa_words = keep.tile([P, GROUPS, K], U32, align_bytes=64)
+        for g in range(GROUPS):
+            load_words(kappa_words[:, g, :], kappa_w_words[g])
+
+        phi_b_sb = keep.tile([P, GROUPS, PACK], BF16)
+        theta_b_sb = keep.tile([P, GROUPS, PACK], BF16)
+        nc.scalar.dma_start(out=phi_b_sb[:], in_=phi_b.rearrange("(g p j) -> p g j", p=P, j=PACK))
+        nc.scalar.dma_start(out=theta_b_sb[:], in_=theta_b.rearrange("(g p j) -> p g j", p=P, j=PACK))
+        lam_bf = keep.tile([P, 1], BF16)
+        nc.scalar.dma_start(out=lam_bf[:], in_=lam.partition_broadcast(P))
+        kappa_b_sb = keep.tile([P, N_TILES], BF16)
+        with nc.allow_non_contiguous_dma(reason="1024 bias values, one to a partition and tile"):
+            nc.scalar.dma_start(out=kappa_b_sb[:], in_=kappa_b.rearrange("(i m) -> m i", m=P))
+        a_bf = keep.tile([P, N_TILES, V * V], BF16)
+        a_rows = A.rearrange("(i m) u v -> m i (u v)", m=P)
+        for pair in range(N_TILES // 2):
+            nc.scalar.dma_start(out=a_bf[:, 2 * pair : 2 * pair + 2, :], in_=a_rows[:, 2 * pair : 2 * pair + 2, :])
+
+        ident = keep.tile([P, P], F32)
+        masks.make_identity(nc, ident[:])
+
+        lam_f = keep.tile([P, 1], F32)
+        nc.vector.tensor_copy(out=lam_f[:], in_=lam_bf[:])
+        lam_kappa_b = keep.tile([P, N_TILES], F32)
+        nc.vector.tensor_scalar_mul(out=lam_kappa_b[:], in0=kappa_b_sb[:], scalar1=lam_f[:, 0:1])
+        bias_diff = keep.tile([P, GROUPS, PACK], F32)
+        nc.vector.tensor_sub(out=bias_diff[:], in0=phi_b_sb[:], in1=theta_b_sb[:])
+        bias_t = keep.tile([P, GROUPS, PACK], F32)
+        nc.vector.tensor_scalar_mul(out=bias_t[:], in0=bias_diff[:], scalar1=float(T))
+
+        x_words = x_sb[:].bitcast(F32)
+        x_grouped = keep.tile([P, T, B, V, PACK], BF16, align_bytes=64)
+        x_grouped_words = x_grouped[:].bitcast(F32)
+        for b in range(B):
+            x_t = banks.tile([P, 2, 2, P], F32, name="x_t", tag="bank")
+            for t_high in range(2):
+                for s in range(2):
+                    nc.tensor.transpose(x_t[:, t_high, s, :], x_words[:, 2 * b + t_high, s : C // 2 : 2], ident[:])
+            for t_high in range(2):
+                src = x_t[:, t_high].rearrange("p s (t v) -> p t v s", v=V)
+                dst = x_grouped_words[:, 4 * t_high : 4 * t_high + 4, b, :, :]
+                if b % 2 == 0:
+                    nc.vector.tensor_copy(out=dst, in_=src)
+                else:
+                    nc.scalar.copy(out=dst, in_=src)
+        x_codes = keep.tile([P, T, ROWS], U32, align_bytes=64)
+        x_scales = keep.tile([P, T, ROWS], U8, align_bytes=64)
+        for half in range(2):
+            steps = slice(4 * half, 4 * half + 4)
+            nc.vector.quantize_mx(
+                out=x_codes[:, steps, :].rearrange("p t r -> p (t r)").bitcast(FP8X4),
+                scales=x_scales[:, steps, :].rearrange("p t r -> p (t r)"),
+                in_=x_grouped[:, steps].rearrange("p t b v j -> p (t b v j)"),
+            )
+
+        a_plus = keep.tile([P, N_TILES, V * V], F32)
+        for i in range(N_TILES):
+            if i % 2 == 0:
+                nc.scalar.activation(
+                    out=a_plus[:, i, :], in_=a_bf[:, i, :], func=ACT.Identity, bias=lam_kappa_b[:, i : i + 1], scale=1.0
+                )
+            else:
+                nc.vector.tensor_scalar_add(out=a_plus[:, i, :], in0=a_bf[:, i, :], scalar1=lam_kappa_b[:, i : i + 1])
+
+        p_sb = keep.tile([P, GROUPS, ROWS, PACK], F32)
+        th_sb = keep.tile([P, GROUPS, ROWS, PACK], F32)
+        th_t = []
+        for g in range(GROUPS):
+            channels = slice(K_PASS * g, K_PASS * (g + 1))
+            sorted_sums = []
+            for name, words, first_row in (("phi", phi_words, PHI_ROW), ("theta", theta_words, THETA_ROW)):
+                sums = banks.tile([P, K_PASS], F32, name="sums", tag="bank")
+                for t in range(T):
+                    nc.tensor.matmul_mx(
+                        out=sums[:],
+                        lhsT=x_codes[:, t, :].bitcast(FP8X4),
+                        lhsT_scale=x_scales[:, t, :],
+                        rhs=words[:, channels].bitcast(FP8X4),
+                        rhs_scale=planes[first_row:P, channels],
+                        start=(t == 0),
+                        stop=(t == T - 1),
+                    )
+                by_j = keep.tile([P, PACK, P], F32, name="by_j_%s%d" % (name, g))
+                src = sums[:].rearrange("r (p j) -> r j p", j=PACK)
+                if name == "phi":
+                    nc.vector.tensor_copy(out=by_j[:], in_=src)
+                else:
+                    nc.scalar.copy(out=by_j[:], in_=src)
+                sorted_sums.append(by_j)
+            p_t = banks.tile([P, PACK, ROWS], F32, name="p_t", tag="bank")
+            th_t.append(th_banks.tile([P, PACK, ROWS], F32, name="th_t%d" % g))
+            for j in range(PACK):
+                nc.tensor.transpose(p_t[:, j, :], sorted_sums[0][:, j, :], ident[:])
+            for j in range(PACK):
+                nc.tensor.transpose(th_t[g][:, j, :], sorted_sums[1][:, j, :], ident[:])
+            nc.vector.tensor_tensor(
+                out=p_sb[:, g],
+                in0=p_t[:].rearrange("p j r -> p r j"),
+                in1=bias_t[:, g, :].unsqueeze(1).to_broadcast([P, ROWS, PACK]),
+                op=ALU.add,
+            )
+            nc.scalar.copy(out=th_sb[:, g], in_=th_t[g][:].rearrange("p j r -> p r j"))
+
+        def make_f(chunk, g, f_codes, f_scales):
+            b = chunk * U_CHUNK // V
+            first_u = chunk * U_CHUNK
+            joints = slice(V * b, V * (b + 1))
+            diff = diff_pool.tile([P, U_CHUNK, V, PACK], F32, name="diff")
+            nc.vector.tensor_tensor(
+                out=diff[:, :U_VECTOR],
+                in0=p_sb[:, g, first_u : first_u + U_VECTOR, :].unsqueeze(2).to_broadcast([P, U_VECTOR, V, PACK]),
+                in1=th_t[g][:, :, joints].rearrange("p j v -> p v j").unsqueeze(1).to_broadcast([P, U_VECTOR, V, PACK]),
+                op=ALU.subtract,
+            )
+            u_rest = U_CHUNK - U_VECTOR
+            nc.gpsimd.tensor_tensor(
+                out=diff[:, U_VECTOR:],
+                in0=p_sb[:, g, first_u + U_VECTOR : first_u + U_CHUNK, :].unsqueeze(2).to_broadcast([P, u_rest, V, PACK]),
+                in1=th_sb[:, g, joints, :].unsqueeze(1).to_broadcast([P, u_rest, V, PACK]),
+                op=ALU.subtract,
+            )
+            f_bf = f_pool.tile([P, CHUNK * PACK], BF16, name="f_bf", align_bytes=64)
+            nc.scalar.activation(
+                out=f_bf[:], in_=diff[:].rearrange("p u v j -> p (u v j)"), func=ACT.Tanh, scale=1.0 / T
+            )
+            nc.vector.quantize_mx(out=f_codes[:, g, :].bitcast(FP8X4), scales=f_scales[:, g, :], in_=f_bf[:])
+
+        def finish(chunk, f_codes, f_scales):
+            b = chunk * U_CHUNK // V
+            u_in_b = chunk * U_CHUNK % V
+            columns = slice(u_in_b * V, u_in_b * V + CHUNK)
+            for i in range(N_TILES):
+                n_cols = slice(P * i, P * (i + 1))
+                g_t = banks.tile([P, CHUNK], F32, name="g_t", tag="bank")
+                for g in range(GROUPS):
+                    nc.tensor.matmul_mx(
+                        out=g_t[:],
+                        lhsT=kappa_words[:, g, n_cols].bitcast(FP8X4),
+                        lhsT_scale=planes[KAPPA_ROW + 4 * g : P, n_cols],
+                        rhs=f_codes[:, g, :].bitcast(FP8X4),
+                        rhs_scale=f_scales[:, g, :],
+                        start=(g == 0),
+                        stop=(g == GROUPS - 1),
+                    )
+                result = out_pool.tile([P, CHUNK], F32, name="result")
+                nc.vector.scalar_tensor_tensor(
+                    out=result[:], in0=g_t[:], scalar=lam_f[:, 0:1], in1=a_plus[:, i, columns], op0=ALU.mult, op1=ALU.add
+                )
+                nc.sync.dma_start(
+                    out=out[b, n_cols, u_in_b : u_in_b + U_CHUNK, :].rearrange("n u v -> n (u v)"), in_=result[:]
+                )
+
+        for chunk in range(CHUNKS):
+            f_codes = code_pool.tile([P, GROUPS, CHUNK], U32, name="f_codes", align_bytes=64)
+            f_scales = code_pool.tile([P, GROUPS, CHUNK], U8, name="f_scales", align_bytes=64)
+            for g in range(GROUPS):
+                make_f(chunk, g, f_codes, f_scales)
+            finish(chunk, f_codes, f_scales)

@@ -19,10 +19,13 @@ B, T, V, C, K = 4, 8, 32, 512, 1024
 GROUPS = K // K_PASS
 N_TILES = K // P
 ROWS = B * V
+T_HALF = T // 2
 U_CHUNK = 16
 CHUNK = U_CHUNK * V
-CHUNKS = B * V // U_CHUNK
+PIECES = (B * V // U_CHUNK) * GROUPS
 U_VECTOR = 6
+AHEAD = 2
+TILES_A_STEP = N_TILES // GROUPS
 
 PHI_ROW, THETA_ROW, KAPPA_ROW = 0, 4, 8
 
@@ -47,21 +50,33 @@ def tile_attgcn_pa_kernel(
 ):
     nc = tc.nc
     with ExitStack() as ctx:
+        ctx.enter_context(tc.manual_schedule())
         keep = ctx.enter_context(tc.tile_pool(name="keep", bufs=1))
-        diff_pool = ctx.enter_context(tc.tile_pool(name="diff_pool", bufs=3))
+        p_pool = ctx.enter_context(tc.tile_pool(name="p_pool", bufs=4))
+        diff_pool = ctx.enter_context(tc.tile_pool(name="diff_pool", bufs=4))
         f_pool = ctx.enter_context(tc.tile_pool(name="f_pool", bufs=3))
-        code_pool = ctx.enter_context(tc.tile_pool(name="code_pool", bufs=3))
-        out_pool = ctx.enter_context(tc.tile_pool(name="out_pool", bufs=6))
-        th_banks = ctx.enter_context(tc.psum_pool(name="th_banks", bufs=1))
-        banks = ctx.enter_context(tc.psum_pool(name="banks", bufs=6))
+        code_pool = ctx.enter_context(tc.tile_pool(name="code_pool", bufs=6))
+        out_pool = ctx.enter_context(tc.tile_pool(name="out_pool", bufs=8))
+        held = ctx.enter_context(tc.psum_pool(name="held", bufs=1))
+        banks = ctx.enter_context(tc.psum_pool(name="banks", bufs=4))
+
+        phi_b_sb = keep.tile([P, GROUPS, PACK], BF16)
+        theta_b_sb = keep.tile([P, GROUPS, PACK], BF16)
+        nc.scalar.dma_start(out=phi_b_sb[:], in_=phi_b.rearrange("(g p j) -> p g j", p=P, j=PACK))
+        nc.scalar.dma_start(out=theta_b_sb[:], in_=theta_b.rearrange("(g p j) -> p g j", p=P, j=PACK))
+        lam_bf = keep.tile([P, 1], BF16)
+        nc.scalar.dma_start(out=lam_bf[:], in_=lam.partition_broadcast(P))
+        kappa_b_sb = keep.tile([P, N_TILES], BF16)
+        with nc.allow_non_contiguous_dma(reason="1024 bias values, one to a partition and tile"):
+            nc.scalar.dma_start(out=kappa_b_sb[:], in_=kappa_b.rearrange("(i m) -> m i", m=P))
 
         planes = keep.tile([P, K], U8, align_bytes=64)
         nc.vector.memset(planes[:].bitcast(I32), 0)
 
-        x_sb = keep.tile([P, B * T * V // P, C], BF16)
-        x_rows = x.rearrange("b t v c -> (b t v) c").rearrange("(r p) c -> p r c", p=P)
-        for half in range(2):
-            nc.sync.dma_start(out=x_sb[:, 4 * half : 4 * half + 4, :], in_=x_rows[:, 4 * half : 4 * half + 4, :])
+        x_sb = keep.tile([P, 2, B, C], BF16)
+        x_tiles = x.rearrange("b (h t) v c -> h (t v) b c", h=2)
+        for h in range(2):
+            nc.sync.dma_start(out=x_sb[:, h], in_=x_tiles[h])
 
         def load_scale_rows(first_row, scales):
             groups = scales.shape[0]
@@ -81,62 +96,51 @@ def tile_attgcn_pa_kernel(
         theta_words = keep.tile([P, K], U32, align_bytes=64)
         load_words(phi_words[:], phi_w_words[0])
         load_words(theta_words[:], theta_w_words[0])
+        a_bf = keep.tile([P, N_TILES, V * V], BF16)
+        a_rows = A.rearrange("(i m) u v -> m i (u v)", m=P)
+        for pair in range(N_TILES // 2):
+            nc.sync.dma_start(out=a_bf[:, 2 * pair : 2 * pair + 2, :], in_=a_rows[:, 2 * pair : 2 * pair + 2, :])
         load_scale_rows(KAPPA_ROW, kappa_w_scales)
         kappa_words = keep.tile([P, GROUPS, K], U32, align_bytes=64)
         for g in range(GROUPS):
             load_words(kappa_words[:, g, :], kappa_w_words[g])
 
-        phi_b_sb = keep.tile([P, GROUPS, PACK], BF16)
-        theta_b_sb = keep.tile([P, GROUPS, PACK], BF16)
-        nc.scalar.dma_start(out=phi_b_sb[:], in_=phi_b.rearrange("(g p j) -> p g j", p=P, j=PACK))
-        nc.scalar.dma_start(out=theta_b_sb[:], in_=theta_b.rearrange("(g p j) -> p g j", p=P, j=PACK))
-        lam_bf = keep.tile([P, 1], BF16)
-        nc.scalar.dma_start(out=lam_bf[:], in_=lam.partition_broadcast(P))
-        kappa_b_sb = keep.tile([P, N_TILES], BF16)
-        with nc.allow_non_contiguous_dma(reason="1024 bias values, one to a partition and tile"):
-            nc.scalar.dma_start(out=kappa_b_sb[:], in_=kappa_b.rearrange("(i m) -> m i", m=P))
-        a_bf = keep.tile([P, N_TILES, V * V], BF16)
-        a_rows = A.rearrange("(i m) u v -> m i (u v)", m=P)
-        for pair in range(N_TILES // 2):
-            nc.scalar.dma_start(out=a_bf[:, 2 * pair : 2 * pair + 2, :], in_=a_rows[:, 2 * pair : 2 * pair + 2, :])
-
         ident = keep.tile([P, P], F32)
         masks.make_identity(nc, ident[:])
 
-        lam_f = keep.tile([P, 1], F32)
-        nc.vector.tensor_copy(out=lam_f[:], in_=lam_bf[:])
-        lam_kappa_b = keep.tile([P, N_TILES], F32)
-        nc.vector.tensor_scalar_mul(out=lam_kappa_b[:], in0=kappa_b_sb[:], scalar1=lam_f[:, 0:1])
-        bias_diff = keep.tile([P, GROUPS, PACK], F32)
-        nc.vector.tensor_sub(out=bias_diff[:], in0=phi_b_sb[:], in1=theta_b_sb[:])
-        bias_t = keep.tile([P, GROUPS, PACK], F32)
-        nc.vector.tensor_scalar_mul(out=bias_t[:], in0=bias_diff[:], scalar1=float(T))
+        warm = keep.tile([P, 2], F32)
+        nc.vector.memset(warm[:], 0.0)
+        nc.scalar.activation(out=warm[:, 1:2], in_=warm[:, 0:1], func=ACT.Tanh)
 
         x_words = x_sb[:].bitcast(F32)
         x_grouped = keep.tile([P, T, B, V, PACK], BF16, align_bytes=64)
         x_grouped_words = x_grouped[:].bitcast(F32)
-        for b in range(B):
-            x_t = banks.tile([P, 2, 2, P], F32, name="x_t", tag="bank")
-            for t_high in range(2):
-                for s in range(2):
-                    nc.tensor.transpose(x_t[:, t_high, s, :], x_words[:, 2 * b + t_high, s : C // 2 : 2], ident[:])
-            for t_high in range(2):
-                src = x_t[:, t_high].rearrange("p s (t v) -> p t v s", v=V)
-                dst = x_grouped_words[:, 4 * t_high : 4 * t_high + 4, b, :, :]
-                if b % 2 == 0:
-                    nc.vector.tensor_copy(out=dst, in_=src)
-                else:
-                    nc.scalar.copy(out=dst, in_=src)
         x_codes = keep.tile([P, T, ROWS], U32, align_bytes=64)
         x_scales = keep.tile([P, T, ROWS], U8, align_bytes=64)
-        for half in range(2):
-            steps = slice(4 * half, 4 * half + 4)
+        for h in range(2):
+            steps = slice(T_HALF * h, T_HALF * (h + 1))
+            for pair in range(B // 2):
+                x_t = banks.tile([P, 2, 2, P], F32, name="x_t", tag="bank")
+                for b_low in range(2):
+                    for s in range(2):
+                        nc.tensor.transpose(x_t[:, b_low, s, :], x_words[:, h, 2 * pair + b_low, s : C // 2 : 2], ident[:])
+                for b_low in range(2):
+                    src = x_t[:, b_low].rearrange("p s (t v) -> p t v s", v=V)
+                    dst = x_grouped_words[:, steps, 2 * pair + b_low, :, :]
+                    if pair == 0:
+                        nc.vector.tensor_copy(out=dst, in_=src)
+                    else:
+                        nc.scalar.copy(out=dst, in_=src)
             nc.vector.quantize_mx(
                 out=x_codes[:, steps, :].rearrange("p t r -> p (t r)").bitcast(FP8X4),
                 scales=x_scales[:, steps, :].rearrange("p t r -> p (t r)"),
                 in_=x_grouped[:, steps].rearrange("p t b v j -> p (t b v j)"),
             )
 
+        lam_f = keep.tile([P, 1], F32)
+        nc.vector.tensor_copy(out=lam_f[:], in_=lam_bf[:])
+        lam_kappa_b = keep.tile([P, N_TILES], F32)
+        nc.vector.tensor_scalar_mul(out=lam_kappa_b[:], in0=kappa_b_sb[:], scalar1=lam_f[:, 0:1])
         a_plus = keep.tile([P, N_TILES, V * V], F32)
         for i in range(N_TILES):
             if i % 2 == 0:
@@ -145,75 +149,98 @@ def tile_attgcn_pa_kernel(
                 )
             else:
                 nc.vector.tensor_scalar_add(out=a_plus[:, i, :], in0=a_bf[:, i, :], scalar1=lam_kappa_b[:, i : i + 1])
+        bias_diff = keep.tile([P, GROUPS, PACK], F32)
+        nc.vector.tensor_sub(out=bias_diff[:], in0=phi_b_sb[:], in1=theta_b_sb[:])
+        bias_t = keep.tile([P, GROUPS, PACK], F32)
+        nc.vector.tensor_scalar_mul(out=bias_t[:], in0=bias_diff[:], scalar1=float(T))
 
-        p_sb = keep.tile([P, GROUPS, ROWS, PACK], F32)
-        th_sb = keep.tile([P, GROUPS, ROWS, PACK], F32)
-        th_t = []
-        for g in range(GROUPS):
+        by_j = {}
+
+        def sum_over_t(name, g, words, first_row):
             channels = slice(K_PASS * g, K_PASS * (g + 1))
-            sorted_sums = []
-            for name, words, first_row in (("phi", phi_words, PHI_ROW), ("theta", theta_words, THETA_ROW)):
-                sums = banks.tile([P, K_PASS], F32, name="sums", tag="bank")
-                for t in range(T):
-                    nc.tensor.matmul_mx(
-                        out=sums[:],
-                        lhsT=x_codes[:, t, :].bitcast(FP8X4),
-                        lhsT_scale=x_scales[:, t, :],
-                        rhs=words[:, channels].bitcast(FP8X4),
-                        rhs_scale=planes[first_row:P, channels],
-                        start=(t == 0),
-                        stop=(t == T - 1),
-                    )
-                by_j = keep.tile([P, PACK, P], F32, name="by_j_%s%d" % (name, g))
-                src = sums[:].rearrange("r (p j) -> r j p", j=PACK)
-                if name == "phi":
-                    nc.vector.tensor_copy(out=by_j[:], in_=src)
-                else:
-                    nc.scalar.copy(out=by_j[:], in_=src)
-                sorted_sums.append(by_j)
-            p_t = banks.tile([P, PACK, ROWS], F32, name="p_t", tag="bank")
-            th_t.append(th_banks.tile([P, PACK, ROWS], F32, name="th_t%d" % g))
+            sums = banks.tile([P, K_PASS], F32, name="sums", tag="bank")
+            for t in range(T):
+                nc.tensor.matmul_mx(
+                    out=sums[:],
+                    lhsT=x_codes[:, t, :].bitcast(FP8X4),
+                    lhsT_scale=x_scales[:, t, :],
+                    rhs=words[:, channels].bitcast(FP8X4),
+                    rhs_scale=planes[first_row:P, channels],
+                    start=(t == 0),
+                    stop=(t == T - 1),
+                )
+            by_j[name, g] = keep.tile([P, PACK, P], F32, name="by_j_%s%d" % (name, g))
+            src = sums[:].rearrange("r (p j) -> r j p", j=PACK)
+            if name == "phi":
+                nc.vector.tensor_copy(out=by_j[name, g][:], in_=src)
+            else:
+                nc.scalar.copy(out=by_j[name, g][:], in_=src)
+
+        p_t = {}
+        th_t = {}
+        th_sb = keep.tile([P, GROUPS, ROWS, PACK], F32)
+
+        def channels_to_partitions(g):
+            p_t[g] = held.tile([P, PACK, ROWS], F32, name="p_t%d" % g)
+            th_t[g] = held.tile([P, PACK, ROWS], F32, name="th_t%d" % g)
             for j in range(PACK):
-                nc.tensor.transpose(p_t[:, j, :], sorted_sums[0][:, j, :], ident[:])
+                nc.tensor.transpose(p_t[g][:, j, :], by_j["phi", g][:, j, :], ident[:])
             for j in range(PACK):
-                nc.tensor.transpose(th_t[g][:, j, :], sorted_sums[1][:, j, :], ident[:])
-            nc.vector.tensor_tensor(
-                out=p_sb[:, g],
-                in0=p_t[:].rearrange("p j r -> p r j"),
-                in1=bias_t[:, g, :].unsqueeze(1).to_broadcast([P, ROWS, PACK]),
-                op=ALU.add,
-            )
+                nc.tensor.transpose(th_t[g][:, j, :], by_j["theta", g][:, j, :], ident[:])
             nc.scalar.copy(out=th_sb[:, g], in_=th_t[g][:].rearrange("p j r -> p r j"))
 
-        def make_f(chunk, g, f_codes, f_scales):
-            b = chunk * U_CHUNK // V
+        sum_over_t("phi", 0, phi_words, PHI_ROW)
+        sum_over_t("theta", 0, theta_words, THETA_ROW)
+        sum_over_t("phi", 1, phi_words, PHI_ROW)
+        channels_to_partitions(0)
+        sum_over_t("theta", 1, theta_words, THETA_ROW)
+        channels_to_partitions(1)
+
+        f_bf = {}
+        f_codes = {}
+        f_scales = {}
+
+        def subtract_and_tanh(piece):
+            chunk, g = divmod(piece, GROUPS)
             first_u = chunk * U_CHUNK
+            b = first_u // V
             joints = slice(V * b, V * (b + 1))
-            diff = diff_pool.tile([P, U_CHUNK, V, PACK], F32, name="diff")
+            p_piece = p_pool.tile([P, U_CHUNK, PACK], F32, name="p_piece")
             nc.vector.tensor_tensor(
-                out=diff[:, :U_VECTOR],
-                in0=p_sb[:, g, first_u : first_u + U_VECTOR, :].unsqueeze(2).to_broadcast([P, U_VECTOR, V, PACK]),
-                in1=th_t[g][:, :, joints].rearrange("p j v -> p v j").unsqueeze(1).to_broadcast([P, U_VECTOR, V, PACK]),
-                op=ALU.subtract,
+                out=p_piece[:],
+                in0=p_t[g][:, :, first_u : first_u + U_CHUNK].rearrange("p j u -> p u j"),
+                in1=bias_t[:, g, :].unsqueeze(1).to_broadcast([P, U_CHUNK, PACK]),
+                op=ALU.add,
             )
+            diff = diff_pool.tile([P, U_CHUNK, V, PACK], F32, name="diff")
             u_rest = U_CHUNK - U_VECTOR
             nc.gpsimd.tensor_tensor(
                 out=diff[:, U_VECTOR:],
-                in0=p_sb[:, g, first_u + U_VECTOR : first_u + U_CHUNK, :].unsqueeze(2).to_broadcast([P, u_rest, V, PACK]),
+                in0=p_piece[:, U_VECTOR:, :].unsqueeze(2).to_broadcast([P, u_rest, V, PACK]),
                 in1=th_sb[:, g, joints, :].unsqueeze(1).to_broadcast([P, u_rest, V, PACK]),
                 op=ALU.subtract,
             )
-            f_bf = f_pool.tile([P, CHUNK * PACK], BF16, name="f_bf", align_bytes=64)
-            nc.scalar.activation(
-                out=f_bf[:], in_=diff[:].rearrange("p u v j -> p (u v j)"), func=ACT.Tanh, scale=1.0 / T
+            nc.vector.tensor_tensor(
+                out=diff[:, :U_VECTOR],
+                in0=p_piece[:, :U_VECTOR, :].unsqueeze(2).to_broadcast([P, U_VECTOR, V, PACK]),
+                in1=th_t[g][:, :, joints].rearrange("p j v -> p v j").unsqueeze(1).to_broadcast([P, U_VECTOR, V, PACK]),
+                op=ALU.subtract,
             )
-            nc.vector.quantize_mx(out=f_codes[:, g, :].bitcast(FP8X4), scales=f_scales[:, g, :], in_=f_bf[:])
+            f_bf[piece] = f_pool.tile([P, CHUNK * PACK], BF16, name="f_bf", align_bytes=64)
+            nc.scalar.activation(
+                out=f_bf[piece][:], in_=diff[:].rearrange("p u v j -> p (u v j)"), func=ACT.Tanh, scale=1.0 / T
+            )
 
-        def finish(chunk, f_codes, f_scales):
+        def quantise(piece):
+            f_codes[piece] = code_pool.tile([P, CHUNK], U32, name="f_codes", align_bytes=64)
+            f_scales[piece] = code_pool.tile([P, CHUNK], U8, name="f_scales", align_bytes=64)
+            nc.vector.quantize_mx(out=f_codes[piece][:].bitcast(FP8X4), scales=f_scales[piece][:], in_=f_bf[piece][:])
+
+        def finish(chunk, first_tile):
             b = chunk * U_CHUNK // V
             u_in_b = chunk * U_CHUNK % V
             columns = slice(u_in_b * V, u_in_b * V + CHUNK)
-            for i in range(N_TILES):
+            for i in range(first_tile, first_tile + TILES_A_STEP):
                 n_cols = slice(P * i, P * (i + 1))
                 g_t = banks.tile([P, CHUNK], F32, name="g_t", tag="bank")
                 for g in range(GROUPS):
@@ -221,8 +248,8 @@ def tile_attgcn_pa_kernel(
                         out=g_t[:],
                         lhsT=kappa_words[:, g, n_cols].bitcast(FP8X4),
                         lhsT_scale=planes[KAPPA_ROW + 4 * g : P, n_cols],
-                        rhs=f_codes[:, g, :].bitcast(FP8X4),
-                        rhs_scale=f_scales[:, g, :],
+                        rhs=f_codes[GROUPS * chunk + g][:].bitcast(FP8X4),
+                        rhs_scale=f_scales[GROUPS * chunk + g][:],
                         start=(g == 0),
                         stop=(g == GROUPS - 1),
                     )
@@ -234,9 +261,13 @@ def tile_attgcn_pa_kernel(
                     out=out[b, n_cols, u_in_b : u_in_b + U_CHUNK, :].rearrange("n u v -> n (u v)"), in_=result[:]
                 )
 
-        for chunk in range(CHUNKS):
-            f_codes = code_pool.tile([P, GROUPS, CHUNK], U32, name="f_codes", align_bytes=64)
-            f_scales = code_pool.tile([P, GROUPS, CHUNK], U8, name="f_scales", align_bytes=64)
-            for g in range(GROUPS):
-                make_f(chunk, g, f_codes, f_scales)
-            finish(chunk, f_codes, f_scales)
+        for piece in range(AHEAD):
+            subtract_and_tanh(piece)
+        for piece in range(PIECES + 1):
+            if piece < PIECES:
+                quantise(piece)
+            if piece + AHEAD < PIECES:
+                subtract_and_tanh(piece + AHEAD)
+            if piece >= 1:
+                chunk, second_half = divmod(piece - 1, GROUPS)
+                finish(chunk, TILES_A_STEP * second_half)

@@ -23,7 +23,7 @@ T_HALF = T // 2
 U_CHUNK = 16
 CHUNK = U_CHUNK * V
 PIECES = (B * V // U_CHUNK) * GROUPS
-U_VECTOR = 6
+U_VECTOR = 8
 AHEAD = 2
 TILES_A_STEP = N_TILES // GROUPS
 

@@ -22,9 +22,9 @@ ROWS = B * V
 T_HALF = T // 2
 U_CHUNK = 16
 CHUNK = U_CHUNK * V
-PIECES = (B * V // U_CHUNK) * GROUPS
-U_VECTOR = 8
-AHEAD = 2
+CHUNKS = B * V // U_CHUNK
+PIECES = CHUNKS * GROUPS
+COLS_VECTOR = 128
 TILES_A_STEP = N_TILES // GROUPS
 
 PHI_ROW, THETA_ROW, KAPPA_ROW = 0, 4, 8
@@ -52,23 +52,11 @@ def tile_attgcn_pa_kernel(
     with ExitStack() as ctx:
         ctx.enter_context(tc.manual_schedule())
         keep = ctx.enter_context(tc.tile_pool(name="keep", bufs=1))
-        p_pool = ctx.enter_context(tc.tile_pool(name="p_pool", bufs=4))
-        diff_pool = ctx.enter_context(tc.tile_pool(name="diff_pool", bufs=4))
-        f_pool = ctx.enter_context(tc.tile_pool(name="f_pool", bufs=3))
+        plane_pool = ctx.enter_context(tc.tile_pool(name="plane_pool", bufs=3))
+        grouped_pool = ctx.enter_context(tc.tile_pool(name="grouped_pool", bufs=1))
         code_pool = ctx.enter_context(tc.tile_pool(name="code_pool", bufs=6))
         out_pool = ctx.enter_context(tc.tile_pool(name="out_pool", bufs=8))
-        held = ctx.enter_context(tc.psum_pool(name="held", bufs=1))
-        banks = ctx.enter_context(tc.psum_pool(name="banks", bufs=4))
-
-        phi_b_sb = keep.tile([P, GROUPS, PACK], BF16)
-        theta_b_sb = keep.tile([P, GROUPS, PACK], BF16)
-        nc.scalar.dma_start(out=phi_b_sb[:], in_=phi_b.rearrange("(g p j) -> p g j", p=P, j=PACK))
-        nc.scalar.dma_start(out=theta_b_sb[:], in_=theta_b.rearrange("(g p j) -> p g j", p=P, j=PACK))
-        lam_bf = keep.tile([P, 1], BF16)
-        nc.scalar.dma_start(out=lam_bf[:], in_=lam.partition_broadcast(P))
-        kappa_b_sb = keep.tile([P, N_TILES], BF16)
-        with nc.allow_non_contiguous_dma(reason="1024 bias values, one to a partition and tile"):
-            nc.scalar.dma_start(out=kappa_b_sb[:], in_=kappa_b.rearrange("(i m) -> m i", m=P))
+        banks = ctx.enter_context(tc.psum_pool(name="banks", bufs=8))
 
         planes = keep.tile([P, K], U8, align_bytes=64)
         nc.vector.memset(planes[:].bitcast(I32), 0)
@@ -104,6 +92,16 @@ def tile_attgcn_pa_kernel(
         kappa_words = keep.tile([P, GROUPS, K], U32, align_bytes=64)
         for g in range(GROUPS):
             load_words(kappa_words[:, g, :], kappa_w_words[g])
+
+        phi_b_sb = keep.tile([P, GROUPS, PACK], BF16)
+        theta_b_sb = keep.tile([P, GROUPS, PACK], BF16)
+        nc.scalar.dma_start(out=phi_b_sb[:], in_=phi_b.rearrange("(g p j) -> p g j", p=P, j=PACK))
+        nc.scalar.dma_start(out=theta_b_sb[:], in_=theta_b.rearrange("(g p j) -> p g j", p=P, j=PACK))
+        lam_bf = keep.tile([P, 1], BF16)
+        nc.scalar.dma_start(out=lam_bf[:], in_=lam.partition_broadcast(P))
+        kappa_b_sb = keep.tile([P, N_TILES], BF16)
+        with nc.allow_non_contiguous_dma(reason="1024 bias values, one to a partition and tile"):
+            nc.scalar.dma_start(out=kappa_b_sb[:], in_=kappa_b.rearrange("(i m) -> m i", m=P))
 
         ident = keep.tile([P, P], F32)
         masks.make_identity(nc, ident[:])
@@ -141,18 +139,18 @@ def tile_attgcn_pa_kernel(
         nc.vector.tensor_copy(out=lam_f[:], in_=lam_bf[:])
         lam_kappa_b = keep.tile([P, N_TILES], F32)
         nc.vector.tensor_scalar_mul(out=lam_kappa_b[:], in0=kappa_b_sb[:], scalar1=lam_f[:, 0:1])
-        a_plus = keep.tile([P, N_TILES, V * V], F32)
-        for i in range(N_TILES):
-            if i % 2 == 0:
-                nc.scalar.activation(
-                    out=a_plus[:, i, :], in_=a_bf[:, i, :], func=ACT.Identity, bias=lam_kappa_b[:, i : i + 1], scale=1.0
-                )
-            else:
-                nc.vector.tensor_scalar_add(out=a_plus[:, i, :], in0=a_bf[:, i, :], scalar1=lam_kappa_b[:, i : i + 1])
         bias_diff = keep.tile([P, GROUPS, PACK], F32)
         nc.vector.tensor_sub(out=bias_diff[:], in0=phi_b_sb[:], in1=theta_b_sb[:])
-        bias_t = keep.tile([P, GROUPS, PACK], F32)
-        nc.vector.tensor_scalar_mul(out=bias_t[:], in0=bias_diff[:], scalar1=float(T))
+        a_plus = keep.tile([P, N_TILES, V * V], F32)
+        for i in range(N_TILES):
+            nc.gpsimd.tensor_scalar(
+                out=a_plus[:, i, :],
+                in0=a_bf[:, i, :],
+                scalar1=1.0,
+                scalar2=lam_kappa_b[:, i : i + 1],
+                op0=ALU.mult,
+                op1=ALU.add,
+            )
 
         by_j = {}
 
@@ -176,98 +174,114 @@ def tile_attgcn_pa_kernel(
             else:
                 nc.scalar.copy(out=by_j[name, g][:], in_=src)
 
-        p_t = {}
-        th_t = {}
-        th_sb = keep.tile([P, GROUPS, ROWS, PACK], F32)
+        p_sb = keep.tile([P, GROUPS, PACK, ROWS], F32)
+        th_sum = keep.tile([P, GROUPS, PACK, ROWS], F32)
 
         def channels_to_partitions(g):
-            p_t[g] = held.tile([P, PACK, ROWS], F32, name="p_t%d" % g)
-            th_t[g] = held.tile([P, PACK, ROWS], F32, name="th_t%d" % g)
+            p_t = banks.tile([P, PACK, ROWS], F32, name="p_t", tag="bank")
+            th_t = banks.tile([P, PACK, ROWS], F32, name="th_t", tag="bank")
             for j in range(PACK):
-                nc.tensor.transpose(p_t[g][:, j, :], by_j["phi", g][:, j, :], ident[:])
+                nc.tensor.transpose(p_t[:, j, :], by_j["phi", g][:, j, :], ident[:])
             for j in range(PACK):
-                nc.tensor.transpose(th_t[g][:, j, :], by_j["theta", g][:, j, :], ident[:])
-            nc.scalar.copy(out=th_sb[:, g], in_=th_t[g][:].rearrange("p j r -> p r j"))
+                nc.tensor.transpose(th_t[:, j, :], by_j["theta", g][:, j, :], ident[:])
+            nc.vector.scalar_tensor_tensor(
+                out=p_sb[:, g],
+                in0=p_t[:],
+                scalar=1.0 / T,
+                in1=bias_diff[:, g, :].unsqueeze(2).to_broadcast([P, PACK, ROWS]),
+                op0=ALU.mult,
+                op1=ALU.add,
+            )
+            nc.scalar.copy(out=th_sum[:, g], in_=th_t[:])
 
-        sum_over_t("phi", 0, phi_words, PHI_ROW)
-        sum_over_t("theta", 0, theta_words, THETA_ROW)
-        sum_over_t("phi", 1, phi_words, PHI_ROW)
-        channels_to_partitions(0)
-        sum_over_t("theta", 1, theta_words, THETA_ROW)
-        channels_to_partitions(1)
-
-        f_bf = {}
+        f_planes = {}
         f_codes = {}
         f_scales = {}
+        g_t = {}
 
-        def subtract_and_tanh(piece):
+        def tanh_planes(piece):
             chunk, g = divmod(piece, GROUPS)
             first_u = chunk * U_CHUNK
             b = first_u // V
-            joints = slice(V * b, V * (b + 1))
-            p_piece = p_pool.tile([P, U_CHUNK, PACK], F32, name="p_piece")
-            nc.vector.tensor_tensor(
-                out=p_piece[:],
-                in0=p_t[g][:, :, first_u : first_u + U_CHUNK].rearrange("p j u -> p u j"),
-                in1=bias_t[:, g, :].unsqueeze(1).to_broadcast([P, U_CHUNK, PACK]),
-                op=ALU.add,
-            )
-            diff = diff_pool.tile([P, U_CHUNK, V, PACK], F32, name="diff")
-            u_rest = U_CHUNK - U_VECTOR
-            nc.gpsimd.tensor_tensor(
-                out=diff[:, U_VECTOR:],
-                in0=p_piece[:, U_VECTOR:, :].unsqueeze(2).to_broadcast([P, u_rest, V, PACK]),
-                in1=th_sb[:, g, joints, :].unsqueeze(1).to_broadcast([P, u_rest, V, PACK]),
-                op=ALU.subtract,
-            )
-            nc.vector.tensor_tensor(
-                out=diff[:, :U_VECTOR],
-                in0=p_piece[:, :U_VECTOR, :].unsqueeze(2).to_broadcast([P, U_VECTOR, V, PACK]),
-                in1=th_t[g][:, :, joints].rearrange("p j v -> p v j").unsqueeze(1).to_broadcast([P, U_VECTOR, V, PACK]),
-                op=ALU.subtract,
-            )
-            f_bf[piece] = f_pool.tile([P, CHUNK * PACK], BF16, name="f_bf", align_bytes=64)
-            nc.scalar.activation(
-                out=f_bf[piece][:], in_=diff[:].rearrange("p u v j -> p (u v j)"), func=ACT.Tanh, scale=1.0 / T
-            )
+            f_planes[piece] = plane_pool.tile([P, PACK, CHUNK], BF16, name="f_planes")
+            for j in range(PACK):
+                for u in range(U_CHUNK):
+                    nc.scalar.activation(
+                        out=f_planes[piece][:, j, V * u : V * (u + 1)],
+                        in_=th_sum[:, g, j, V * b : V * (b + 1)],
+                        func=ACT.Tanh,
+                        bias=p_sb[:, g, j, first_u + u : first_u + u + 1],
+                        scale=-1.0 / T,
+                    )
 
         def quantise(piece):
+            f_grouped = grouped_pool.tile([P, CHUNK, PACK], BF16, name="f_grouped", align_bytes=64)
+            by_column = f_planes[piece][:].rearrange("p j c -> p c j")
+            nc.gpsimd.tensor_scalar(
+                out=f_grouped[:, COLS_VECTOR:, :],
+                in0=by_column[:, COLS_VECTOR:, :],
+                scalar1=1.0,
+                scalar2=0.0,
+                op0=ALU.mult,
+                op1=ALU.add,
+            )
+            nc.vector.tensor_copy(out=f_grouped[:, :COLS_VECTOR, :], in_=by_column[:, :COLS_VECTOR, :])
             f_codes[piece] = code_pool.tile([P, CHUNK], U32, name="f_codes", align_bytes=64)
             f_scales[piece] = code_pool.tile([P, CHUNK], U8, name="f_scales", align_bytes=64)
-            nc.vector.quantize_mx(out=f_codes[piece][:].bitcast(FP8X4), scales=f_scales[piece][:], in_=f_bf[piece][:])
+            nc.vector.quantize_mx(
+                out=f_codes[piece][:].bitcast(FP8X4),
+                scales=f_scales[piece][:],
+                in_=f_grouped[:].rearrange("p c j -> p (c j)"),
+            )
 
-        def finish(chunk, first_tile):
+        def multiply(tile_no):
+            chunk, i = divmod(tile_no, N_TILES)
+            n_cols = slice(P * i, P * (i + 1))
+            g_t[tile_no] = banks.tile([P, CHUNK], F32, name="g_t", tag="bank")
+            for g in range(GROUPS):
+                nc.tensor.matmul_mx(
+                    out=g_t[tile_no][:],
+                    lhsT=kappa_words[:, g, n_cols].bitcast(FP8X4),
+                    lhsT_scale=planes[KAPPA_ROW + 4 * g : P, n_cols],
+                    rhs=f_codes[GROUPS * chunk + g][:].bitcast(FP8X4),
+                    rhs_scale=f_scales[GROUPS * chunk + g][:],
+                    start=(g == 0),
+                    stop=(g == GROUPS - 1),
+                )
+
+        def finish(tile_no):
+            chunk, i = divmod(tile_no, N_TILES)
             b = chunk * U_CHUNK // V
             u_in_b = chunk * U_CHUNK % V
-            columns = slice(u_in_b * V, u_in_b * V + CHUNK)
-            for i in range(first_tile, first_tile + TILES_A_STEP):
-                n_cols = slice(P * i, P * (i + 1))
-                g_t = banks.tile([P, CHUNK], F32, name="g_t", tag="bank")
-                for g in range(GROUPS):
-                    nc.tensor.matmul_mx(
-                        out=g_t[:],
-                        lhsT=kappa_words[:, g, n_cols].bitcast(FP8X4),
-                        lhsT_scale=planes[KAPPA_ROW + 4 * g : P, n_cols],
-                        rhs=f_codes[GROUPS * chunk + g][:].bitcast(FP8X4),
-                        rhs_scale=f_scales[GROUPS * chunk + g][:],
-                        start=(g == 0),
-                        stop=(g == GROUPS - 1),
-                    )
-                result = out_pool.tile([P, CHUNK], F32, name="result")
-                nc.vector.scalar_tensor_tensor(
-                    out=result[:], in0=g_t[:], scalar=lam_f[:, 0:1], in1=a_plus[:, i, columns], op0=ALU.mult, op1=ALU.add
-                )
-                nc.sync.dma_start(
-                    out=out[b, n_cols, u_in_b : u_in_b + U_CHUNK, :].rearrange("n u v -> n (u v)"), in_=result[:]
-                )
+            result = out_pool.tile([P, CHUNK], F32, name="result")
+            nc.vector.scalar_tensor_tensor(
+                out=result[:],
+                in0=g_t[tile_no][:],
+                scalar=lam_f[:, 0:1],
+                in1=a_plus[:, i, u_in_b * V : u_in_b * V + CHUNK],
+                op0=ALU.mult,
+                op1=ALU.add,
+            )
+            nc.sync.dma_start(
+                out=out[b, P * i : P * (i + 1), u_in_b : u_in_b + U_CHUNK, :].rearrange("n u v -> n (u v)"),
+                in_=result[:],
+            )
 
-        for piece in range(AHEAD):
-            subtract_and_tanh(piece)
-        for piece in range(PIECES + 1):
+        sum_over_t("phi", 0, phi_words, PHI_ROW)
+        sum_over_t("theta", 0, theta_words, THETA_ROW)
+        channels_to_partitions(0)
+        tanh_planes(0)
+        sum_over_t("phi", 1, phi_words, PHI_ROW)
+        sum_over_t("theta", 1, theta_words, THETA_ROW)
+        channels_to_partitions(1)
+
+        for piece in range(PIECES + 2):
+            if piece + 1 < PIECES:
+                tanh_planes(piece + 1)
             if piece < PIECES:
                 quantise(piece)
-            if piece + AHEAD < PIECES:
-                subtract_and_tanh(piece + AHEAD)
-            if piece >= 1:
-                chunk, second_half = divmod(piece - 1, GROUPS)
-                finish(chunk, TILES_A_STEP * second_half)
+            for tile_no in range(TILES_A_STEP * (piece - 1), TILES_A_STEP * piece):
+                if 0 <= tile_no < CHUNKS * N_TILES:
+                    multiply(tile_no)
+                if 0 <= tile_no - TILES_A_STEP < CHUNKS * N_TILES:
+                    finish(tile_no - TILES_A_STEP)

@@ -24,10 +24,11 @@ U_CHUNK = 16
 CHUNK = U_CHUNK * V
 CHUNKS = B * V // U_CHUNK
 PIECES = CHUNKS * GROUPS
-COLS_VECTOR = 128
+U_BIAS = 8
+PIECES_ALONE = 2
 TILES_A_STEP = N_TILES // GROUPS
 
-PHI_ROW, THETA_ROW, KAPPA_ROW = 0, 4, 8
+PHI_ROW, THETA_ROW, KAPPA_ROW = 0, 4, 0
 
 FLOPS = 2 * (B * T * V) * C * (2 * K) + 2 * (B * V * V) * K * K
 
@@ -53,33 +54,36 @@ def tile_attgcn_pa_kernel(
         ctx.enter_context(tc.manual_schedule())
         keep = ctx.enter_context(tc.tile_pool(name="keep", bufs=1))
         plane_pool = ctx.enter_context(tc.tile_pool(name="plane_pool", bufs=3))
-        grouped_pool = ctx.enter_context(tc.tile_pool(name="grouped_pool", bufs=1))
+        diff_pool = ctx.enter_context(tc.tile_pool(name="diff_pool", bufs=3))
+        grouped_pool = ctx.enter_context(tc.tile_pool(name="grouped_pool", bufs=3))
         code_pool = ctx.enter_context(tc.tile_pool(name="code_pool", bufs=6))
         out_pool = ctx.enter_context(tc.tile_pool(name="out_pool", bufs=8))
         banks = ctx.enter_context(tc.psum_pool(name="banks", bufs=8))
 
         planes = keep.tile([P, K], U8, align_bytes=64)
+        kappa_planes = keep.tile([P, K], U8, align_bytes=64)
         nc.vector.memset(planes[:].bitcast(I32), 0)
+        nc.vector.memset(kappa_planes[:].bitcast(I32), 0)
 
         x_sb = keep.tile([P, 2, B, C], BF16)
         x_tiles = x.rearrange("b (h t) v c -> h (t v) b c", h=2)
         for h in range(2):
             nc.sync.dma_start(out=x_sb[:, h], in_=x_tiles[h])
 
-        def load_scale_rows(first_row, scales):
+        def load_scale_rows(tile, first_row, scales):
             groups = scales.shape[0]
             for quad in range(4):
                 first = 32 * quad + first_row
                 nc.sync.dma_start(
-                    out=planes[first : first + 4 * groups, :].bitcast(I32),
+                    out=tile[first : first + 4 * groups, :].bitcast(I32),
                     in_=scales[:, 4 * quad : 4 * quad + 4, :].bitcast(I32),
                 )
 
         def load_words(words_sb, words):
             nc.sync.dma_start(out=words_sb.bitcast(I32), in_=words.rearrange("p n t -> p (n t)").bitcast(I32))
 
-        load_scale_rows(PHI_ROW, phi_w_scales)
-        load_scale_rows(THETA_ROW, theta_w_scales)
+        load_scale_rows(planes, PHI_ROW, phi_w_scales)
+        load_scale_rows(planes, THETA_ROW, theta_w_scales)
         phi_words = keep.tile([P, K], U32, align_bytes=64)
         theta_words = keep.tile([P, K], U32, align_bytes=64)
         load_words(phi_words[:], phi_w_words[0])
@@ -88,7 +92,7 @@ def tile_attgcn_pa_kernel(
         a_rows = A.rearrange("(i m) u v -> m i (u v)", m=P)
         for pair in range(N_TILES // 2):
             nc.sync.dma_start(out=a_bf[:, 2 * pair : 2 * pair + 2, :], in_=a_rows[:, 2 * pair : 2 * pair + 2, :])
-        load_scale_rows(KAPPA_ROW, kappa_w_scales)
+        load_scale_rows(kappa_planes, KAPPA_ROW, kappa_w_scales)
         kappa_words = keep.tile([P, GROUPS, K], U32, align_bytes=64)
         for g in range(GROUPS):
             load_words(kappa_words[:, g, :], kappa_w_words[g])
@@ -115,6 +119,17 @@ def tile_attgcn_pa_kernel(
         x_grouped_words = x_grouped[:].bitcast(F32)
         x_codes = keep.tile([P, T, ROWS], U32, align_bytes=64)
         x_scales = keep.tile([P, T, ROWS], U8, align_bytes=64)
+        phi_sorted = keep.tile([P, GROUPS, PACK, P], U32, align_bytes=64)
+        theta_sorted = keep.tile([P, GROUPS, PACK, P], U32, align_bytes=64)
+        planes_sorted = keep.tile([P, GROUPS, PACK, P], U8, align_bytes=64)
+
+        def sort_columns(g):
+            for dst, src in ((phi_sorted, phi_words), (theta_sorted, theta_words), (planes_sorted, planes)):
+                out_ap, in_ap = dst[:, g], src[:, K_PASS * g : K_PASS * (g + 1)]
+                if src is not planes:
+                    out_ap, in_ap = out_ap.bitcast(I32), in_ap.bitcast(I32)
+                nc.vector.tensor_copy(out=out_ap, in_=in_ap.rearrange("p (m j) -> p j m", j=PACK))
+
         for h in range(2):
             steps = slice(T_HALF * h, T_HALF * (h + 1))
             for pair in range(B // 2):
@@ -125,15 +140,16 @@ def tile_attgcn_pa_kernel(
                 for b_low in range(2):
                     src = x_t[:, b_low].rearrange("p s (t v) -> p t v s", v=V)
                     dst = x_grouped_words[:, steps, 2 * pair + b_low, :, :]
-                    if pair == 0:
-                        nc.vector.tensor_copy(out=dst, in_=src)
-                    else:
-                        nc.scalar.copy(out=dst, in_=src)
+                    nc.scalar.copy(out=dst, in_=src)
             nc.vector.quantize_mx(
                 out=x_codes[:, steps, :].rearrange("p t r -> p (t r)").bitcast(FP8X4),
                 scales=x_scales[:, steps, :].rearrange("p t r -> p (t r)"),
                 in_=x_grouped[:, steps].rearrange("p t b v j -> p (t b v j)"),
             )
+            if h == 0:
+                sort_columns(0)
+
+        sort_columns(1)
 
         lam_f = keep.tile([P, 1], F32)
         nc.vector.tensor_copy(out=lam_f[:], in_=lam_bf[:])
@@ -152,86 +168,93 @@ def tile_attgcn_pa_kernel(
                 op1=ALU.add,
             )
 
-        by_j = {}
-
-        def sum_over_t(name, g, words, first_row):
-            channels = slice(K_PASS * g, K_PASS * (g + 1))
-            sums = banks.tile([P, K_PASS], F32, name="sums", tag="bank")
-            for t in range(T):
-                nc.tensor.matmul_mx(
-                    out=sums[:],
-                    lhsT=x_codes[:, t, :].bitcast(FP8X4),
-                    lhsT_scale=x_scales[:, t, :],
-                    rhs=words[:, channels].bitcast(FP8X4),
-                    rhs_scale=planes[first_row:P, channels],
-                    start=(t == 0),
-                    stop=(t == T - 1),
-                )
-            by_j[name, g] = keep.tile([P, PACK, P], F32, name="by_j_%s%d" % (name, g))
-            src = sums[:].rearrange("r (p j) -> r j p", j=PACK)
-            if name == "phi":
-                nc.vector.tensor_copy(out=by_j[name, g][:], in_=src)
-            else:
-                nc.scalar.copy(out=by_j[name, g][:], in_=src)
-
         p_sb = keep.tile([P, GROUPS, PACK, ROWS], F32)
-        th_sum = keep.tile([P, GROUPS, PACK, ROWS], F32)
+        th_sb = keep.tile([P, GROUPS, PACK, ROWS], F32)
+        p_by_row = keep.tile([P, GROUPS, ROWS, PACK], F32)
+        th_by_row = keep.tile([P, GROUPS, ROWS, PACK], F32)
 
-        def channels_to_partitions(g):
-            p_t = banks.tile([P, PACK, ROWS], F32, name="p_t", tag="bank")
-            th_t = banks.tile([P, PACK, ROWS], F32, name="th_t", tag="bank")
-            for j in range(PACK):
-                nc.tensor.transpose(p_t[:, j, :], by_j["phi", g][:, j, :], ident[:])
-            for j in range(PACK):
-                nc.tensor.transpose(th_t[:, j, :], by_j["theta", g][:, j, :], ident[:])
-            nc.vector.scalar_tensor_tensor(
-                out=p_sb[:, g],
-                in0=p_t[:],
-                scalar=1.0 / T,
-                in1=bias_diff[:, g, :].unsqueeze(2).to_broadcast([P, PACK, ROWS]),
+        def sort_by_row(g):
+            for dst, src in ((th_by_row, th_sb), (p_by_row, p_sb)):
+                nc.vector.tensor_copy(out=dst[:, g], in_=src[:, g].rearrange("p j r -> p r j"))
+
+        def sum_over_t(g, j):
+            sums = banks.tile([P, 2, ROWS], F32, name="sums", tag="bank")
+            for side, (words, first_row) in enumerate(((phi_sorted, PHI_ROW), (theta_sorted, THETA_ROW))):
+                for t in range(T):
+                    nc.tensor.matmul_mx(
+                        out=sums[:, side, :],
+                        lhsT=words[:, g, j, :].bitcast(FP8X4),
+                        lhsT_scale=planes_sorted[first_row:P, g, j, :],
+                        rhs=x_codes[:, t, :].bitcast(FP8X4),
+                        rhs_scale=x_scales[:, t, :],
+                        start=(t == 0),
+                        stop=(t == T - 1),
+                    )
+            nc.vector.tensor_scalar(
+                out=p_sb[:, g, j, :],
+                in0=sums[:, 0, :],
+                scalar1=1.0 / T,
+                scalar2=bias_diff[:, g, j : j + 1],
                 op0=ALU.mult,
                 op1=ALU.add,
             )
-            nc.scalar.copy(out=th_sum[:, g], in_=th_t[:])
+            nc.vector.tensor_scalar_mul(out=th_sb[:, g, j, :], in0=sums[:, 1, :], scalar1=1.0 / T)
 
         f_planes = {}
+        f_grouped = {}
+        diffs = {}
         f_codes = {}
         f_scales = {}
         g_t = {}
+        cols_bias = U_BIAS * V
+        u_diff = U_CHUNK - U_BIAS
 
-        def tanh_planes(piece):
+        def subtract(piece):
+            chunk, g = divmod(piece, GROUPS)
+            first_u = chunk * U_CHUNK + U_BIAS
+            b = first_u // V
+            diffs[piece] = diff_pool.tile([P, u_diff, V, PACK], F32, name="diffs")
+            engine = nc.vector if piece < PIECES_ALONE else nc.gpsimd
+            engine.tensor_tensor(
+                out=diffs[piece][:],
+                in0=p_by_row[:, g, first_u : first_u + u_diff, :].unsqueeze(2).to_broadcast([P, u_diff, V, PACK]),
+                in1=th_by_row[:, g, V * b : V * (b + 1), :].unsqueeze(1).to_broadcast([P, u_diff, V, PACK]),
+                op=ALU.subtract,
+            )
+
+        def tanh_piece(piece):
             chunk, g = divmod(piece, GROUPS)
             first_u = chunk * U_CHUNK
             b = first_u // V
-            f_planes[piece] = plane_pool.tile([P, PACK, CHUNK], BF16, name="f_planes")
+            f_planes[piece] = plane_pool.tile([P, PACK, cols_bias], BF16, name="f_planes")
+            f_grouped[piece] = grouped_pool.tile([P, CHUNK, PACK], BF16, name="f_grouped", align_bytes=64)
             for j in range(PACK):
-                for u in range(U_CHUNK):
+                for u in range(U_BIAS):
                     nc.scalar.activation(
                         out=f_planes[piece][:, j, V * u : V * (u + 1)],
-                        in_=th_sum[:, g, j, V * b : V * (b + 1)],
+                        in_=th_sb[:, g, j, V * b : V * (b + 1)],
                         func=ACT.Tanh,
                         bias=p_sb[:, g, j, first_u + u : first_u + u + 1],
-                        scale=-1.0 / T,
+                        scale=-1.0,
                     )
+            nc.scalar.activation(
+                out=f_grouped[piece][:, cols_bias:, :].rearrange("p c j -> p (c j)"),
+                in_=diffs[piece][:].rearrange("p u v j -> p (u v j)"),
+                func=ACT.Tanh,
+            )
+
+        def regroup(piece):
+            nc.vector.tensor_copy(
+                out=f_grouped[piece][:, :cols_bias, :], in_=f_planes[piece][:].rearrange("p j c -> p c j")
+            )
 
         def quantise(piece):
-            f_grouped = grouped_pool.tile([P, CHUNK, PACK], BF16, name="f_grouped", align_bytes=64)
-            by_column = f_planes[piece][:].rearrange("p j c -> p c j")
-            nc.gpsimd.tensor_scalar(
-                out=f_grouped[:, COLS_VECTOR:, :],
-                in0=by_column[:, COLS_VECTOR:, :],
-                scalar1=1.0,
-                scalar2=0.0,
-                op0=ALU.mult,
-                op1=ALU.add,
-            )
-            nc.vector.tensor_copy(out=f_grouped[:, :COLS_VECTOR, :], in_=by_column[:, :COLS_VECTOR, :])
             f_codes[piece] = code_pool.tile([P, CHUNK], U32, name="f_codes", align_bytes=64)
             f_scales[piece] = code_pool.tile([P, CHUNK], U8, name="f_scales", align_bytes=64)
             nc.vector.quantize_mx(
                 out=f_codes[piece][:].bitcast(FP8X4),
                 scales=f_scales[piece][:],
-                in_=f_grouped[:].rearrange("p c j -> p (c j)"),
+                in_=f_grouped[piece][:].rearrange("p c j -> p (c j)"),
             )
 
         def multiply(tile_no):
@@ -242,7 +265,7 @@ def tile_attgcn_pa_kernel(
                 nc.tensor.matmul_mx(
                     out=g_t[tile_no][:],
                     lhsT=kappa_words[:, g, n_cols].bitcast(FP8X4),
-                    lhsT_scale=planes[KAPPA_ROW + 4 * g : P, n_cols],
+                    lhsT_scale=kappa_planes[KAPPA_ROW + 4 * g : P, n_cols],
                     rhs=f_codes[GROUPS * chunk + g][:].bitcast(FP8X4),
                     rhs_scale=f_scales[GROUPS * chunk + g][:],
                     start=(g == 0),
@@ -267,21 +290,29 @@ def tile_attgcn_pa_kernel(
                 in_=result[:],
             )
 
-        sum_over_t("phi", 0, phi_words, PHI_ROW)
-        sum_over_t("theta", 0, theta_words, THETA_ROW)
-        channels_to_partitions(0)
-        tanh_planes(0)
-        sum_over_t("phi", 1, phi_words, PHI_ROW)
-        sum_over_t("theta", 1, theta_words, THETA_ROW)
-        channels_to_partitions(1)
+        for j in range(PACK):
+            sum_over_t(0, j)
+        sort_by_row(0)
+        subtract(0)
+        tanh_piece(0)
+        for j in range(PACK):
+            sum_over_t(1, j)
+        sort_by_row(1)
+        subtract(1)
 
         for piece in range(PIECES + 2):
+            if piece + 2 < PIECES:
+                subtract(piece + 2)
             if piece + 1 < PIECES:
-                tanh_planes(piece + 1)
+                tanh_piece(piece + 1)
             if piece < PIECES:
-                quantise(piece)
-            for tile_no in range(TILES_A_STEP * (piece - 1), TILES_A_STEP * piece):
+                regroup(piece)
+            tiles = range(TILES_A_STEP * (piece - 1), TILES_A_STEP * piece)
+            for n, tile_no in enumerate(tiles):
+                if 0 <= tile_no - TILES_A_STEP:
+                    finish(tile_no - TILES_A_STEP)
+                if n == 1 and piece < PIECES:
+                    quantise(piece)
+            for tile_no in tiles:
                 if 0 <= tile_no < CHUNKS * N_TILES:
                     multiply(tile_no)
-                if 0 <= tile_no - TILES_A_STEP < CHUNKS * N_TILES:
-                    finish(tile_no - TILES_A_STEP)

@@ -24,8 +24,9 @@ U_CHUNK = 16
 CHUNK = U_CHUNK * V
 CHUNKS = B * V // U_CHUNK
 PIECES = CHUNKS * GROUPS
-U_BIAS = 8
-PIECES_ALONE = 2
+U_BIAS = 9
+PIECES_BIAS = 2
+LEAD = 4
 TILES_A_STEP = N_TILES // GROUPS
 
 PHI_ROW, THETA_ROW, KAPPA_ROW = 0, 4, 0
@@ -82,12 +83,15 @@ def tile_attgcn_pa_kernel(
         def load_words(words_sb, words):
             nc.sync.dma_start(out=words_sb.bitcast(I32), in_=words.rearrange("p n t -> p (n t)").bitcast(I32))
 
-        load_scale_rows(planes, PHI_ROW, phi_w_scales)
-        load_scale_rows(planes, THETA_ROW, theta_w_scales)
         phi_words = keep.tile([P, K], U32, align_bytes=64)
         theta_words = keep.tile([P, K], U32, align_bytes=64)
-        load_words(phi_words[:], phi_w_words[0])
-        load_words(theta_words[:], theta_w_words[0])
+        for g in range(GROUPS):
+            channels = slice(K_PASS * g, K_PASS * (g + 1))
+            load_words(phi_words[:, channels], phi_w_words[0, :, channels, :])
+            load_words(theta_words[:, channels], theta_w_words[0, :, channels, :])
+            if g == 0:
+                load_scale_rows(planes, PHI_ROW, phi_w_scales)
+                load_scale_rows(planes, THETA_ROW, theta_w_scales)
         a_bf = keep.tile([P, N_TILES, V * V], BF16)
         a_rows = A.rearrange("(i m) u v -> m i (u v)", m=P)
         for pair in range(N_TILES // 2):
@@ -123,12 +127,20 @@ def tile_attgcn_pa_kernel(
         theta_sorted = keep.tile([P, GROUPS, PACK, P], U32, align_bytes=64)
         planes_sorted = keep.tile([P, GROUPS, PACK, P], U8, align_bytes=64)
 
-        def sort_columns(g):
-            for dst, src in ((phi_sorted, phi_words), (theta_sorted, theta_words), (planes_sorted, planes)):
-                out_ap, in_ap = dst[:, g], src[:, K_PASS * g : K_PASS * (g + 1)]
-                if src is not planes:
-                    out_ap, in_ap = out_ap.bitcast(I32), in_ap.bitcast(I32)
-                nc.vector.tensor_copy(out=out_ap, in_=in_ap.rearrange("p (m j) -> p j m", j=PACK))
+        def sort_words(g):
+            for dst, src in ((phi_sorted, phi_words), (theta_sorted, theta_words)):
+                nc.vector.tensor_copy(
+                    out=dst[:, g].bitcast(I32),
+                    in_=src[:, K_PASS * g : K_PASS * (g + 1)].bitcast(I32).rearrange("p (m j) -> p j m", j=PACK),
+                )
+
+        def sort_planes(g):
+            nc.vector.tensor_copy(
+                out=planes_sorted[:, g],
+                in_=planes[:, K_PASS * g : K_PASS * (g + 1)].rearrange("p (m j) -> p j m", j=PACK),
+            )
+
+        sort_words(0)
 
         for h in range(2):
             steps = slice(T_HALF * h, T_HALF * (h + 1))
@@ -147,9 +159,7 @@ def tile_attgcn_pa_kernel(
                 in_=x_grouped[:, steps].rearrange("p t b v j -> p (t b v j)"),
             )
             if h == 0:
-                sort_columns(0)
-
-        sort_columns(1)
+                sort_planes(0)
 
         lam_f = keep.tile([P, 1], F32)
         nc.vector.tensor_copy(out=lam_f[:], in_=lam_bf[:])
@@ -157,9 +167,12 @@ def tile_attgcn_pa_kernel(
         nc.vector.tensor_scalar_mul(out=lam_kappa_b[:], in0=kappa_b_sb[:], scalar1=lam_f[:, 0:1])
         bias_diff = keep.tile([P, GROUPS, PACK], F32)
         nc.vector.tensor_sub(out=bias_diff[:], in0=phi_b_sb[:], in1=theta_b_sb[:])
+        sort_words(1)
+        sort_planes(1)
         a_plus = keep.tile([P, N_TILES, V * V], F32)
-        for i in range(N_TILES):
-            nc.gpsimd.tensor_scalar(
+
+        def prepare_a(i):
+            nc.vector.tensor_scalar(
                 out=a_plus[:, i, :],
                 in0=a_bf[:, i, :],
                 scalar1=1.0,
@@ -171,11 +184,9 @@ def tile_attgcn_pa_kernel(
         p_sb = keep.tile([P, GROUPS, PACK, ROWS], F32)
         th_sb = keep.tile([P, GROUPS, PACK, ROWS], F32)
         p_by_row = keep.tile([P, GROUPS, ROWS, PACK], F32)
-        th_by_row = keep.tile([P, GROUPS, ROWS, PACK], F32)
 
-        def sort_by_row(g):
-            for dst, src in ((th_by_row, th_sb), (p_by_row, p_sb)):
-                nc.vector.tensor_copy(out=dst[:, g], in_=src[:, g].rearrange("p j r -> p r j"))
+        def sort_p_by_row(g):
+            nc.vector.tensor_copy(out=p_by_row[:, g], in_=p_sb[:, g].rearrange("p j r -> p r j"))
 
         def sum_over_t(g, j):
             sums = banks.tile([P, 2, ROWS], F32, name="sums", tag="bank")
@@ -202,34 +213,48 @@ def tile_attgcn_pa_kernel(
 
         f_planes = {}
         f_grouped = {}
+        th_now = {}
         diffs = {}
         f_codes = {}
         f_scales = {}
         g_t = {}
-        cols_bias = U_BIAS * V
-        u_diff = U_CHUNK - U_BIAS
+
+        def joints_by_bias(piece):
+            return U_CHUNK if piece < PIECES_BIAS else U_BIAS
+
+        def hand_over(piece):
+            chunk, g = divmod(piece, GROUPS)
+            b = chunk * U_CHUNK // V
+            th_now[piece] = diff_pool.tile([P, V, PACK], F32, name="th_now")
+            nc.vector.tensor_copy(
+                out=th_now[piece][:], in_=th_sb[:, g, :, V * b : V * (b + 1)].rearrange("p j v -> p v j")
+            )
 
         def subtract(piece):
             chunk, g = divmod(piece, GROUPS)
+            u_diff = U_CHUNK - U_BIAS
             first_u = chunk * U_CHUNK + U_BIAS
-            b = first_u // V
             diffs[piece] = diff_pool.tile([P, u_diff, V, PACK], F32, name="diffs")
-            engine = nc.vector if piece < PIECES_ALONE else nc.gpsimd
-            engine.tensor_tensor(
+            nc.gpsimd.tensor_tensor(
                 out=diffs[piece][:],
                 in0=p_by_row[:, g, first_u : first_u + u_diff, :].unsqueeze(2).to_broadcast([P, u_diff, V, PACK]),
-                in1=th_by_row[:, g, V * b : V * (b + 1), :].unsqueeze(1).to_broadcast([P, u_diff, V, PACK]),
+                in1=th_now[piece][:].unsqueeze(1).to_broadcast([P, u_diff, V, PACK]),
                 op=ALU.subtract,
             )
+
+        def start_difference(piece):
+            hand_over(piece)
+            subtract(piece)
 
         def tanh_piece(piece):
             chunk, g = divmod(piece, GROUPS)
             first_u = chunk * U_CHUNK
             b = first_u // V
-            f_planes[piece] = plane_pool.tile([P, PACK, cols_bias], BF16, name="f_planes")
+            u_bias = joints_by_bias(piece)
+            f_planes[piece] = plane_pool.tile([P, PACK, u_bias * V], BF16, name="f_planes")
             f_grouped[piece] = grouped_pool.tile([P, CHUNK, PACK], BF16, name="f_grouped", align_bytes=64)
             for j in range(PACK):
-                for u in range(U_BIAS):
+                for u in range(u_bias):
                     nc.scalar.activation(
                         out=f_planes[piece][:, j, V * u : V * (u + 1)],
                         in_=th_sb[:, g, j, V * b : V * (b + 1)],
@@ -237,16 +262,19 @@ def tile_attgcn_pa_kernel(
                         bias=p_sb[:, g, j, first_u + u : first_u + u + 1],
                         scale=-1.0,
                     )
-            nc.scalar.activation(
-                out=f_grouped[piece][:, cols_bias:, :].rearrange("p c j -> p (c j)"),
-                in_=diffs[piece][:].rearrange("p u v j -> p (u v j)"),
-                func=ACT.Tanh,
-            )
+            if u_bias < U_CHUNK:
+                nc.scalar.activation(
+                    out=f_grouped[piece][:, u_bias * V :, :].rearrange("p c j -> p (c j)"),
+                    in_=diffs[piece][:].rearrange("p u v j -> p (u v j)"),
+                    func=ACT.Tanh,
+                )
 
         def regroup(piece):
-            nc.vector.tensor_copy(
-                out=f_grouped[piece][:, :cols_bias, :], in_=f_planes[piece][:].rearrange("p j c -> p c j")
-            )
+            half = joints_by_bias(piece) * V // 2
+            for cols in (slice(0, half), slice(half, 2 * half)) if piece < PIECES_BIAS else (slice(0, 2 * half),):
+                nc.vector.tensor_copy(
+                    out=f_grouped[piece][:, cols, :], in_=f_planes[piece][:, :, cols].rearrange("p j c -> p c j")
+                )
 
         def quantise(piece):
             f_codes[piece] = code_pool.tile([P, CHUNK], U32, name="f_codes", align_bytes=64)
@@ -272,6 +300,10 @@ def tile_attgcn_pa_kernel(
                     stop=(g == GROUPS - 1),
                 )
 
+        def multiply_four(step):
+            for tile_no in range(TILES_A_STEP * (step - 1), TILES_A_STEP * step):
+                multiply(tile_no)
+
         def finish(tile_no):
             chunk, i = divmod(tile_no, N_TILES)
             b = chunk * U_CHUNK // V
@@ -292,27 +324,40 @@ def tile_attgcn_pa_kernel(
 
         for j in range(PACK):
             sum_over_t(0, j)
-        sort_by_row(0)
-        subtract(0)
+            prepare_a(j)
+        sort_p_by_row(0)
+        start_difference(2)
         tanh_piece(0)
-        for j in range(PACK):
+        sum_over_t(1, 0)
+        regroup(0)
+        quantise(0)
+        for j in range(1, PACK):
             sum_over_t(1, j)
-        sort_by_row(1)
-        subtract(1)
+            prepare_a(PACK + j)
+        tanh_piece(1)
+        tanh_piece(2)
+        regroup(1)
+        sort_p_by_row(1)
+        start_difference(3)
+        quantise(1)
+        multiply_four(1)
+        prepare_a(PACK)
+        start_difference(4)
+        tanh_piece(3)
+        regroup(2)
 
-        for piece in range(PIECES + 2):
+        for piece in range(2, PIECES + 2):
             if piece + 2 < PIECES:
-                subtract(piece + 2)
-            if piece + 1 < PIECES:
-                tanh_piece(piece + 1)
+                tanh_piece(piece + 2)
+            if LEAD <= piece < PIECES - 1:
+                regroup(piece + 1)
             if piece < PIECES:
-                regroup(piece)
-            tiles = range(TILES_A_STEP * (piece - 1), TILES_A_STEP * piece)
-            for n, tile_no in enumerate(tiles):
-                if 0 <= tile_no - TILES_A_STEP:
-                    finish(tile_no - TILES_A_STEP)
-                if n == 1 and piece < PIECES:
-                    quantise(piece)
-            for tile_no in tiles:
-                if 0 <= tile_no < CHUNKS * N_TILES:
-                    multiply(tile_no)
+                quantise(piece)
+            if piece + 3 < PIECES:
+                start_difference(piece + 3)
+            for tile_no in range(TILES_A_STEP * (piece - 2), TILES_A_STEP * (piece - 1)):
+                finish(tile_no)
+            if piece <= PIECES:
+                multiply_four(piece)
+            if piece < LEAD:
+                regroup(piece + 1)

@@ -24,7 +24,8 @@ U_CHUNK = 16
 CHUNK = U_CHUNK * V
 CHUNKS = B * V // U_CHUNK
 PIECES = CHUNKS * GROUPS
-U_BIAS = 9
+U_PE = 4
+U_BIAS = U_CHUNK - U_PE
 PIECES_BIAS = 2
 LEAD = 4
 TILES_A_STEP = N_TILES // GROUPS
@@ -55,11 +56,11 @@ def tile_attgcn_pa_kernel(
         ctx.enter_context(tc.manual_schedule())
         keep = ctx.enter_context(tc.tile_pool(name="keep", bufs=1))
         plane_pool = ctx.enter_context(tc.tile_pool(name="plane_pool", bufs=3))
-        diff_pool = ctx.enter_context(tc.tile_pool(name="diff_pool", bufs=3))
         grouped_pool = ctx.enter_context(tc.tile_pool(name="grouped_pool", bufs=3))
         code_pool = ctx.enter_context(tc.tile_pool(name="code_pool", bufs=6))
         out_pool = ctx.enter_context(tc.tile_pool(name="out_pool", bufs=8))
-        banks = ctx.enter_context(tc.psum_pool(name="banks", bufs=8))
+        banks = ctx.enter_context(tc.psum_pool(name="banks", bufs=6))
+        diff_banks = ctx.enter_context(tc.psum_pool(name="diff_banks", bufs=2))
 
         planes = keep.tile([P, K], U8, align_bytes=64)
         kappa_planes = keep.tile([P, K], U8, align_bytes=64)
@@ -113,6 +114,17 @@ def tile_attgcn_pa_kernel(
 
         ident = keep.tile([P, P], F32)
         masks.make_identity(nc, ident[:])
+        spread = keep.tile([P, 2, 2, U_PE, V], F32)
+        for b_low in range(2):
+            for half in range(2):
+                row_p = 2 * V * b_low + U_CHUNK * (half + 1) - U_PE
+                row_th = 2 * V * b_low + V
+                nc.gpsimd.tensor_tensor(
+                    out=spread[:, b_low, half],
+                    in0=ident[:, row_p : row_p + U_PE].unsqueeze(2).to_broadcast([P, U_PE, V]),
+                    in1=ident[:, row_th : row_th + V].unsqueeze(1).to_broadcast([P, U_PE, V]),
+                    op=ALU.subtract,
+                )
 
         warm = keep.tile([P, 2], F32)
         nc.vector.memset(warm[:], 0.0)
@@ -181,12 +193,18 @@ def tile_attgcn_pa_kernel(
                 op1=ALU.add,
             )
 
-        p_sb = keep.tile([P, GROUPS, PACK, ROWS], F32)
-        th_sb = keep.tile([P, GROUPS, PACK, ROWS], F32)
-        p_by_row = keep.tile([P, GROUPS, ROWS, PACK], F32)
+        p_th = keep.tile([P, GROUPS, PACK, B, 2, V], F32)
+        rows = keep.tile([P, GROUPS, 2, PACK, P], F32)
 
-        def sort_p_by_row(g):
-            nc.vector.tensor_copy(out=p_by_row[:, g], in_=p_sb[:, g].rearrange("p j r -> p r j"))
+        def transpose_rows(g, b_high):
+            rows_t = banks.tile([P, PACK, P], F32, name="rows_t", tag="bank")
+            for j in range(PACK):
+                nc.tensor.transpose(
+                    rows_t[:, j, :],
+                    p_th[:, g, j, 2 * b_high : 2 * b_high + 2].rearrange("p b s v -> p (b s v)"),
+                    ident[:],
+                )
+            nc.vector.tensor_copy(out=rows[:, g, b_high], in_=rows_t[:])
 
         def sum_over_t(g, j):
             sums = banks.tile([P, 2, ROWS], F32, name="sums", tag="bank")
@@ -202,18 +220,19 @@ def tile_attgcn_pa_kernel(
                         stop=(t == T - 1),
                     )
             nc.vector.tensor_scalar(
-                out=p_sb[:, g, j, :],
-                in0=sums[:, 0, :],
+                out=p_th[:, g, j, :, 0, :],
+                in0=sums[:, 0, :].rearrange("p (b v) -> p b v", v=V),
                 scalar1=1.0 / T,
                 scalar2=bias_diff[:, g, j : j + 1],
                 op0=ALU.mult,
                 op1=ALU.add,
             )
-            nc.vector.tensor_scalar_mul(out=th_sb[:, g, j, :], in0=sums[:, 1, :], scalar1=1.0 / T)
+            nc.vector.tensor_scalar_mul(
+                out=p_th[:, g, j, :, 1, :], in0=sums[:, 1, :].rearrange("p (b v) -> p b v", v=V), scalar1=1.0 / T
+            )
 
         f_planes = {}
         f_grouped = {}
-        th_now = {}
         diffs = {}
         f_codes = {}
         f_scales = {}
@@ -222,34 +241,22 @@ def tile_attgcn_pa_kernel(
         def joints_by_bias(piece):
             return U_CHUNK if piece < PIECES_BIAS else U_BIAS
 
-        def hand_over(piece):
-            chunk, g = divmod(piece, GROUPS)
-            b = chunk * U_CHUNK // V
-            th_now[piece] = diff_pool.tile([P, V, PACK], F32, name="th_now")
-            nc.vector.tensor_copy(
-                out=th_now[piece][:], in_=th_sb[:, g, :, V * b : V * (b + 1)].rearrange("p j v -> p v j")
-            )
-
         def subtract(piece):
             chunk, g = divmod(piece, GROUPS)
-            u_diff = U_CHUNK - U_BIAS
-            first_u = chunk * U_CHUNK + U_BIAS
-            diffs[piece] = diff_pool.tile([P, u_diff, V, PACK], F32, name="diffs")
-            nc.gpsimd.tensor_tensor(
-                out=diffs[piece][:],
-                in0=p_by_row[:, g, first_u : first_u + u_diff, :].unsqueeze(2).to_broadcast([P, u_diff, V, PACK]),
-                in1=th_now[piece][:].unsqueeze(1).to_broadcast([P, u_diff, V, PACK]),
-                op=ALU.subtract,
-            )
-
-        def start_difference(piece):
-            hand_over(piece)
-            subtract(piece)
+            b_high, b_low = divmod(chunk * U_CHUNK // V, 2)
+            diffs[piece] = diff_banks.tile([P, PACK, U_PE * V], F32, name="diffs")
+            for j in range(PACK):
+                nc.tensor.matmul(
+                    out=diffs[piece][:, j, :],
+                    lhsT=rows[:, g, b_high, j, :],
+                    rhs=spread[:, b_low, chunk % 2].rearrange("p u v -> p (u v)"),
+                    start=True,
+                    stop=True,
+                )
 
         def tanh_piece(piece):
             chunk, g = divmod(piece, GROUPS)
-            first_u = chunk * U_CHUNK
-            b = first_u // V
+            b, first_u = divmod(chunk * U_CHUNK, V)
             u_bias = joints_by_bias(piece)
             f_planes[piece] = plane_pool.tile([P, PACK, u_bias * V], BF16, name="f_planes")
             f_grouped[piece] = grouped_pool.tile([P, CHUNK, PACK], BF16, name="f_grouped", align_bytes=64)
@@ -257,15 +264,15 @@ def tile_attgcn_pa_kernel(
                 for u in range(u_bias):
                     nc.scalar.activation(
                         out=f_planes[piece][:, j, V * u : V * (u + 1)],
-                        in_=th_sb[:, g, j, V * b : V * (b + 1)],
+                        in_=p_th[:, g, j, b, 1, :],
                         func=ACT.Tanh,
-                        bias=p_sb[:, g, j, first_u + u : first_u + u + 1],
+                        bias=p_th[:, g, j, b, 0, first_u + u : first_u + u + 1],
                         scale=-1.0,
                     )
             if u_bias < U_CHUNK:
                 nc.scalar.activation(
-                    out=f_grouped[piece][:, u_bias * V :, :].rearrange("p c j -> p (c j)"),
-                    in_=diffs[piece][:].rearrange("p u v j -> p (u v j)"),
+                    out=f_grouped[piece][:, u_bias * V :, :],
+                    in_=diffs[piece][:].rearrange("p j c -> p c j"),
                     func=ACT.Tanh,
                 )
 
@@ -325,8 +332,7 @@ def tile_attgcn_pa_kernel(
         for j in range(PACK):
             sum_over_t(0, j)
             prepare_a(j)
-        sort_p_by_row(0)
-        start_difference(2)
+        transpose_rows(0, 0)
         tanh_piece(0)
         sum_over_t(1, 0)
         regroup(0)
@@ -335,29 +341,33 @@ def tile_attgcn_pa_kernel(
             sum_over_t(1, j)
             prepare_a(PACK + j)
         tanh_piece(1)
+        subtract(2)
         tanh_piece(2)
+        transpose_rows(1, 0)
         regroup(1)
-        sort_p_by_row(1)
-        start_difference(3)
-        quantise(1)
-        multiply_four(1)
         prepare_a(PACK)
-        start_difference(4)
+        quantise(1)
+        subtract(3)
+        multiply_four(1)
         tanh_piece(3)
-        regroup(2)
 
         for piece in range(2, PIECES + 2):
             if piece + 2 < PIECES:
+                subtract(piece + 2)
                 tanh_piece(piece + 2)
-            if LEAD <= piece < PIECES - 1:
-                regroup(piece + 1)
-            if piece < PIECES:
+            tiles = range(TILES_A_STEP * (piece - 2), TILES_A_STEP * (piece - 1))
+            if piece < LEAD:
+                for tile_no in tiles:
+                    finish(tile_no)
+                regroup(piece)
+                transpose_rows(piece - 2, 1)
                 quantise(piece)
-            if piece + 3 < PIECES:
-                start_difference(piece + 3)
-            for tile_no in range(TILES_A_STEP * (piece - 2), TILES_A_STEP * (piece - 1)):
-                finish(tile_no)
+            else:
+                if piece < PIECES:
+                    regroup(piece)
+                for n, tile_no in enumerate(tiles):
+                    if n == 2 and piece < PIECES:
+                        quantise(piece)
+                    finish(tile_no)
             if piece <= PIECES:
                 multiply_four(piece)
-            if piece < LEAD:
-                regroup(piece + 1)

@@ -23,6 +23,7 @@ T_HALF = T // 2
 U_CHUNK = 16
 CHUNK = U_CHUNK * V
 CHUNKS = B * V // U_CHUNK
+COLS_HALF = CHUNK // 2
 PIECES = CHUNKS * GROUPS
 U_PE = 4
 U_BIAS = U_CHUNK - U_PE
@@ -56,6 +57,7 @@ def tile_attgcn_pa_kernel(
         ctx.enter_context(tc.manual_schedule())
         keep = ctx.enter_context(tc.tile_pool(name="keep", bufs=1))
         plane_pool = ctx.enter_context(tc.tile_pool(name="plane_pool", bufs=3))
+        gp_pool = ctx.enter_context(tc.tile_pool(name="gp_pool", bufs=1))
         grouped_pool = ctx.enter_context(tc.tile_pool(name="grouped_pool", bufs=3))
         code_pool = ctx.enter_context(tc.tile_pool(name="code_pool", bufs=6))
         out_pool = ctx.enter_context(tc.tile_pool(name="out_pool", bufs=8))
@@ -184,7 +186,7 @@ def tile_attgcn_pa_kernel(
         a_plus = keep.tile([P, N_TILES, V * V], F32)
 
         def prepare_a(i):
-            nc.vector.tensor_scalar(
+            nc.gpsimd.tensor_scalar(
                 out=a_plus[:, i, :],
                 in0=a_bf[:, i, :],
                 scalar1=1.0,
@@ -192,6 +194,9 @@ def tile_attgcn_pa_kernel(
                 op0=ALU.mult,
                 op1=ALU.add,
             )
+
+        for i in range(N_TILES):
+            prepare_a(i)
 
         p_th = keep.tile([P, GROUPS, PACK, B, 2, V], F32)
         rows = keep.tile([P, GROUPS, 2, PACK, P], F32)
@@ -233,6 +238,7 @@ def tile_attgcn_pa_kernel(
 
         f_planes = {}
         f_grouped = {}
+        f_grouped_gp = {}
         diffs = {}
         f_codes = {}
         f_scales = {}
@@ -259,7 +265,7 @@ def tile_attgcn_pa_kernel(
             b, first_u = divmod(chunk * U_CHUNK, V)
             u_bias = joints_by_bias(piece)
             f_planes[piece] = plane_pool.tile([P, PACK, u_bias * V], BF16, name="f_planes")
-            f_grouped[piece] = grouped_pool.tile([P, CHUNK, PACK], BF16, name="f_grouped", align_bytes=64)
+            f_grouped[piece] = grouped_pool.tile([P, COLS_HALF, PACK], BF16, name="f_grouped", align_bytes=64)
             for j in range(PACK):
                 for u in range(u_bias):
                     nc.scalar.activation(
@@ -271,26 +277,38 @@ def tile_attgcn_pa_kernel(
                     )
             if u_bias < U_CHUNK:
                 nc.scalar.activation(
-                    out=f_grouped[piece][:, u_bias * V :, :],
+                    out=f_grouped[piece][:, u_bias * V - COLS_HALF :, :],
                     in_=diffs[piece][:].rearrange("p j c -> p c j"),
                     func=ACT.Tanh,
                 )
 
-        def regroup(piece):
-            half = joints_by_bias(piece) * V // 2
-            for cols in (slice(0, half), slice(half, 2 * half)) if piece < PIECES_BIAS else (slice(0, 2 * half),):
-                nc.vector.tensor_copy(
-                    out=f_grouped[piece][:, cols, :], in_=f_planes[piece][:, :, cols].rearrange("p j c -> p c j")
+        def regroup_gp(piece):
+            f_grouped_gp[piece] = gp_pool.tile([P, COLS_HALF, PACK], BF16, name="f_grouped_gp", align_bytes=64)
+            src = f_planes[piece][:, :, :COLS_HALF].rearrange("p j c -> p c j")
+            if piece < PIECES_BIAS:
+                nc.vector.tensor_copy(out=f_grouped_gp[piece][:], in_=src)
+            else:
+                nc.gpsimd.tensor_scalar(
+                    out=f_grouped_gp[piece][:], in0=src, scalar1=1.0, scalar2=0.0, op0=ALU.mult, op1=ALU.add
                 )
+
+        def regroup(piece):
+            cols = joints_by_bias(piece) * V - COLS_HALF
+            nc.vector.tensor_copy(
+                out=f_grouped[piece][:, :cols, :], in_=f_planes[piece][:, :, COLS_HALF:].rearrange("p j c -> p c j")
+            )
 
         def quantise(piece):
             f_codes[piece] = code_pool.tile([P, CHUNK], U32, name="f_codes", align_bytes=64)
             f_scales[piece] = code_pool.tile([P, CHUNK], U8, name="f_scales", align_bytes=64)
-            nc.vector.quantize_mx(
-                out=f_codes[piece][:].bitcast(FP8X4),
-                scales=f_scales[piece][:],
-                in_=f_grouped[piece][:].rearrange("p c j -> p (c j)"),
-            )
+            for src, cols in ((f_grouped_gp, slice(0, COLS_HALF)), (f_grouped, slice(COLS_HALF, CHUNK))):
+                nc.vector.quantize_mx(
+                    out=f_codes[piece][:, cols].bitcast(FP8X4),
+                    scales=f_scales[piece][:, cols],
+                    in_=src[piece][:].rearrange("p c j -> p (c j)"),
+                )
+            if PIECES_BIAS <= piece + 1 < PIECES:
+                regroup_gp(piece + 1)
 
         def multiply(tile_no):
             chunk, i = divmod(tile_no, N_TILES)
@@ -331,21 +349,20 @@ def tile_attgcn_pa_kernel(
 
         for j in range(PACK):
             sum_over_t(0, j)
-            prepare_a(j)
         transpose_rows(0, 0)
         tanh_piece(0)
         sum_over_t(1, 0)
+        regroup_gp(0)
         regroup(0)
         quantise(0)
         for j in range(1, PACK):
             sum_over_t(1, j)
-            prepare_a(PACK + j)
         tanh_piece(1)
         subtract(2)
         tanh_piece(2)
         transpose_rows(1, 0)
+        regroup_gp(1)
         regroup(1)
-        prepare_a(PACK)
         quantise(1)
         subtract(3)
         multiply_four(1)
@@ -365,9 +382,8 @@ def tile_attgcn_pa_kernel(
             else:
                 if piece < PIECES:
                     regroup(piece)
-                for n, tile_no in enumerate(tiles):
-                    if n == 2 and piece < PIECES:
-                        quantise(piece)
+                    quantise(piece)
+                for tile_no in tiles:
                     finish(tile_no)
             if piece <= PIECES:
                 multiply_four(piece)

@@ -22,13 +22,14 @@ ROWS = B * V
 T_HALF = T // 2
 U_CHUNK = 16
 CHUNK = U_CHUNK * V
-CHUNKS = B * V // U_CHUNK
-COLS_HALF = CHUNK // 2
-PIECES = CHUNKS * GROUPS
+COLS_GP = CHUNK // 2
+CHUNKS = [(b, u, U_CHUNK) for b in range(B) for u in range(0, V, U_CHUNK)][:-1] + [
+    (B - 1, u, U_CHUNK // 2) for u in range(U_CHUNK, V, U_CHUNK // 2)
+]
+PIECES = len(CHUNKS) * GROUPS
 U_PE = 4
-U_BIAS = U_CHUNK - U_PE
 PIECES_BIAS = 2
-LEAD = 4
+PIECES_HEAD = 4
 TILES_A_STEP = N_TILES // GROUPS
 
 PHI_ROW, THETA_ROW, KAPPA_ROW = 0, 4, 0
@@ -56,9 +57,9 @@ def tile_attgcn_pa_kernel(
     with ExitStack() as ctx:
         ctx.enter_context(tc.manual_schedule())
         keep = ctx.enter_context(tc.tile_pool(name="keep", bufs=1))
-        plane_pool = ctx.enter_context(tc.tile_pool(name="plane_pool", bufs=3))
+        plane_pool = ctx.enter_context(tc.tile_pool(name="plane_pool", bufs=4))
         gp_pool = ctx.enter_context(tc.tile_pool(name="gp_pool", bufs=1))
-        grouped_pool = ctx.enter_context(tc.tile_pool(name="grouped_pool", bufs=3))
+        grouped_pool = ctx.enter_context(tc.tile_pool(name="grouped_pool", bufs=4))
         code_pool = ctx.enter_context(tc.tile_pool(name="code_pool", bufs=6))
         out_pool = ctx.enter_context(tc.tile_pool(name="out_pool", bufs=8))
         banks = ctx.enter_context(tc.psum_pool(name="banks", bufs=6))
@@ -71,12 +72,10 @@ def tile_attgcn_pa_kernel(
 
         x_sb = keep.tile([P, 2, B, C], BF16)
         x_tiles = x.rearrange("b (h t) v c -> h (t v) b c", h=2)
-        for h in range(2):
-            nc.sync.dma_start(out=x_sb[:, h], in_=x_tiles[h])
 
-        def load_scale_rows(tile, first_row, scales):
+        def load_scale_rows(tile, first_row, scales, quads=range(4)):
             groups = scales.shape[0]
-            for quad in range(4):
+            for quad in quads:
                 first = 32 * quad + first_row
                 nc.sync.dma_start(
                     out=tile[first : first + 4 * groups, :].bitcast(I32),
@@ -88,13 +87,27 @@ def tile_attgcn_pa_kernel(
 
         phi_words = keep.tile([P, K], U32, align_bytes=64)
         theta_words = keep.tile([P, K], U32, align_bytes=64)
-        for g in range(GROUPS):
-            channels = slice(K_PASS * g, K_PASS * (g + 1))
-            load_words(phi_words[:, channels], phi_w_words[0, :, channels, :])
-            load_words(theta_words[:, channels], theta_w_words[0, :, channels, :])
-            if g == 0:
-                load_scale_rows(planes, PHI_ROW, phi_w_scales)
-                load_scale_rows(planes, THETA_ROW, theta_w_scales)
+        first_half, second_half = slice(0, K_PASS), slice(K_PASS, K)
+        nc.sync.dma_start(out=x_sb[:, 0], in_=x_tiles[0])
+        load_scale_rows(planes, PHI_ROW, phi_w_scales, range(0, 3))
+        nc.sync.dma_start(out=x_sb[:, 1], in_=x_tiles[1])
+        load_words(phi_words[:, first_half], phi_w_words[0, :, first_half, :])
+        load_scale_rows(planes, PHI_ROW, phi_w_scales, range(3, 4))
+        load_words(theta_words[:, first_half], theta_w_words[0, :, first_half, :])
+        load_scale_rows(planes, THETA_ROW, theta_w_scales)
+
+        phi_b_sb = keep.tile([P, GROUPS, PACK], BF16)
+        theta_b_sb = keep.tile([P, GROUPS, PACK], BF16)
+        nc.sync.dma_start(out=phi_b_sb[:], in_=phi_b.rearrange("(g p j) -> p g j", p=P, j=PACK))
+        nc.sync.dma_start(out=theta_b_sb[:], in_=theta_b.rearrange("(g p j) -> p g j", p=P, j=PACK))
+        load_words(phi_words[:, second_half], phi_w_words[0, :, second_half, :])
+        load_words(theta_words[:, second_half], theta_w_words[0, :, second_half, :])
+        lam_bf = keep.tile([P, 1], BF16)
+        nc.sync.dma_start(out=lam_bf[:], in_=lam.partition_broadcast(P))
+        kappa_b_sb = keep.tile([P, N_TILES], BF16)
+        with nc.allow_non_contiguous_dma(reason="1024 bias values, one to a partition and tile"):
+            nc.sync.dma_start(out=kappa_b_sb[:], in_=kappa_b.rearrange("(i m) -> m i", m=P))
+
         a_bf = keep.tile([P, N_TILES, V * V], BF16)
         a_rows = A.rearrange("(i m) u v -> m i (u v)", m=P)
         for pair in range(N_TILES // 2):
@@ -104,25 +117,16 @@ def tile_attgcn_pa_kernel(
         for g in range(GROUPS):
             load_words(kappa_words[:, g, :], kappa_w_words[g])
 
-        phi_b_sb = keep.tile([P, GROUPS, PACK], BF16)
-        theta_b_sb = keep.tile([P, GROUPS, PACK], BF16)
-        nc.scalar.dma_start(out=phi_b_sb[:], in_=phi_b.rearrange("(g p j) -> p g j", p=P, j=PACK))
-        nc.scalar.dma_start(out=theta_b_sb[:], in_=theta_b.rearrange("(g p j) -> p g j", p=P, j=PACK))
-        lam_bf = keep.tile([P, 1], BF16)
-        nc.scalar.dma_start(out=lam_bf[:], in_=lam.partition_broadcast(P))
-        kappa_b_sb = keep.tile([P, N_TILES], BF16)
-        with nc.allow_non_contiguous_dma(reason="1024 bias values, one to a partition and tile"):
-            nc.scalar.dma_start(out=kappa_b_sb[:], in_=kappa_b.rearrange("(i m) -> m i", m=P))
-
         ident = keep.tile([P, P], F32)
         masks.make_identity(nc, ident[:])
-        spread = keep.tile([P, 2, 2, U_PE, V], F32)
+        spread = {}
         for b_low in range(2):
-            for half in range(2):
-                row_p = 2 * V * b_low + U_CHUNK * (half + 1) - U_PE
+            for u in range(U_CHUNK - U_PE, V, U_CHUNK):
+                spread[b_low, u] = keep.tile([P, U_PE, V], F32, name="spread_%d_%d" % (b_low, u))
+                row_p = 2 * V * b_low + u
                 row_th = 2 * V * b_low + V
                 nc.gpsimd.tensor_tensor(
-                    out=spread[:, b_low, half],
+                    out=spread[b_low, u][:],
                     in0=ident[:, row_p : row_p + U_PE].unsqueeze(2).to_broadcast([P, U_PE, V]),
                     in1=ident[:, row_th : row_th + V].unsqueeze(1).to_broadcast([P, U_PE, V]),
                     op=ALU.subtract,
@@ -141,20 +145,17 @@ def tile_attgcn_pa_kernel(
         theta_sorted = keep.tile([P, GROUPS, PACK, P], U32, align_bytes=64)
         planes_sorted = keep.tile([P, GROUPS, PACK, P], U8, align_bytes=64)
 
-        def sort_words(g):
-            for dst, src in ((phi_sorted, phi_words), (theta_sorted, theta_words)):
-                nc.vector.tensor_copy(
-                    out=dst[:, g].bitcast(I32),
-                    in_=src[:, K_PASS * g : K_PASS * (g + 1)].bitcast(I32).rearrange("p (m j) -> p j m", j=PACK),
-                )
+        def sort_words(dst, src, g):
+            nc.vector.tensor_copy(
+                out=dst[:, g].bitcast(I32),
+                in_=src[:, K_PASS * g : K_PASS * (g + 1)].bitcast(I32).rearrange("p (m j) -> p j m", j=PACK),
+            )
 
         def sort_planes(g):
             nc.vector.tensor_copy(
                 out=planes_sorted[:, g],
                 in_=planes[:, K_PASS * g : K_PASS * (g + 1)].rearrange("p (m j) -> p j m", j=PACK),
             )
-
-        sort_words(0)
 
         for h in range(2):
             steps = slice(T_HALF * h, T_HALF * (h + 1))
@@ -166,14 +167,19 @@ def tile_attgcn_pa_kernel(
                 for b_low in range(2):
                     src = x_t[:, b_low].rearrange("p s (t v) -> p t v s", v=V)
                     dst = x_grouped_words[:, steps, 2 * pair + b_low, :, :]
-                    nc.scalar.copy(out=dst, in_=src)
+                    if pair == 0:
+                        nc.vector.tensor_copy(out=dst, in_=src)
+                    else:
+                        nc.scalar.copy(out=dst, in_=src)
             nc.vector.quantize_mx(
                 out=x_codes[:, steps, :].rearrange("p t r -> p (t r)").bitcast(FP8X4),
                 scales=x_scales[:, steps, :].rearrange("p t r -> p (t r)"),
                 in_=x_grouped[:, steps].rearrange("p t b v j -> p (t b v j)"),
             )
             if h == 0:
+                sort_words(phi_sorted, phi_words, 0)
                 sort_planes(0)
+        sort_words(theta_sorted, theta_words, 0)
 
         lam_f = keep.tile([P, 1], F32)
         nc.vector.tensor_copy(out=lam_f[:], in_=lam_bf[:])
@@ -181,8 +187,6 @@ def tile_attgcn_pa_kernel(
         nc.vector.tensor_scalar_mul(out=lam_kappa_b[:], in0=kappa_b_sb[:], scalar1=lam_f[:, 0:1])
         bias_diff = keep.tile([P, GROUPS, PACK], F32)
         nc.vector.tensor_sub(out=bias_diff[:], in0=phi_b_sb[:], in1=theta_b_sb[:])
-        sort_words(1)
-        sort_planes(1)
         a_plus = keep.tile([P, N_TILES, V * V], F32)
 
         def prepare_a(i):
@@ -209,6 +213,9 @@ def tile_attgcn_pa_kernel(
                     p_th[:, g, j, 2 * b_high : 2 * b_high + 2].rearrange("p b s v -> p (b s v)"),
                     ident[:],
                 )
+            return rows_t
+
+        def copy_rows(g, b_high, rows_t):
             nc.vector.tensor_copy(out=rows[:, g, b_high], in_=rows_t[:])
 
         def sum_over_t(g, j):
@@ -244,76 +251,92 @@ def tile_attgcn_pa_kernel(
         f_scales = {}
         g_t = {}
 
-        def joints_by_bias(piece):
-            return U_CHUNK if piece < PIECES_BIAS else U_BIAS
+        def of_piece(piece):
+            chunk, g = divmod(piece, GROUPS)
+            b, first_u, n_u = CHUNKS[chunk]
+            n_bias = n_u if piece < PIECES_BIAS or n_u < U_CHUNK else n_u - U_PE
+            return b, first_u, n_u, n_bias, g
+
+        def has_differences(piece):
+            return piece < PIECES and of_piece(piece)[3] < of_piece(piece)[2]
+
+        def cols_gp(piece):
+            return COLS_GP if of_piece(piece)[2] == U_CHUNK else 0
 
         def subtract(piece):
-            chunk, g = divmod(piece, GROUPS)
-            b_high, b_low = divmod(chunk * U_CHUNK // V, 2)
+            b, first_u, n_u, n_bias, g = of_piece(piece)
+            b_high, b_low = divmod(b, 2)
             diffs[piece] = diff_banks.tile([P, PACK, U_PE * V], F32, name="diffs")
             for j in range(PACK):
                 nc.tensor.matmul(
                     out=diffs[piece][:, j, :],
                     lhsT=rows[:, g, b_high, j, :],
-                    rhs=spread[:, b_low, chunk % 2].rearrange("p u v -> p (u v)"),
+                    rhs=spread[b_low, first_u + n_bias][:].rearrange("p u v -> p (u v)"),
                     start=True,
                     stop=True,
                 )
 
-        def tanh_piece(piece):
-            chunk, g = divmod(piece, GROUPS)
-            b, first_u = divmod(chunk * U_CHUNK, V)
-            u_bias = joints_by_bias(piece)
-            f_planes[piece] = plane_pool.tile([P, PACK, u_bias * V], BF16, name="f_planes")
-            f_grouped[piece] = grouped_pool.tile([P, COLS_HALF, PACK], BF16, name="f_grouped", align_bytes=64)
-            for j in range(PACK):
-                for u in range(u_bias):
-                    nc.scalar.activation(
-                        out=f_planes[piece][:, j, V * u : V * (u + 1)],
-                        in_=p_th[:, g, j, b, 1, :],
-                        func=ACT.Tanh,
-                        bias=p_th[:, g, j, b, 0, first_u + u : first_u + u + 1],
-                        scale=-1.0,
-                    )
-            if u_bias < U_CHUNK:
+        def tanh_by_bias(piece, j):
+            b, first_u, n_u, n_bias, g = of_piece(piece)
+            if j == 0:
+                f_planes[piece] = plane_pool.tile([P, PACK, n_bias * V], BF16, name="f_planes")
+                f_grouped[piece] = grouped_pool.tile(
+                    [P, n_u * V - cols_gp(piece), PACK], BF16, name="f_grouped", align_bytes=64
+                )
+            for u in range(n_bias):
                 nc.scalar.activation(
-                    out=f_grouped[piece][:, u_bias * V - COLS_HALF :, :],
-                    in_=diffs[piece][:].rearrange("p j c -> p c j"),
+                    out=f_planes[piece][:, j, V * u : V * (u + 1)],
+                    in_=p_th[:, g, j, b, 1, :],
                     func=ACT.Tanh,
+                    bias=p_th[:, g, j, b, 0, first_u + u : first_u + u + 1],
+                    scale=-1.0,
                 )
 
-        def regroup_gp(piece):
-            f_grouped_gp[piece] = gp_pool.tile([P, COLS_HALF, PACK], BF16, name="f_grouped_gp", align_bytes=64)
-            src = f_planes[piece][:, :, :COLS_HALF].rearrange("p j c -> p c j")
-            if piece < PIECES_BIAS:
-                nc.vector.tensor_copy(out=f_grouped_gp[piece][:], in_=src)
-            else:
-                nc.gpsimd.tensor_scalar(
-                    out=f_grouped_gp[piece][:], in0=src, scalar1=1.0, scalar2=0.0, op0=ALU.mult, op1=ALU.add
-                )
-
-        def regroup(piece):
-            cols = joints_by_bias(piece) * V - COLS_HALF
-            nc.vector.tensor_copy(
-                out=f_grouped[piece][:, :cols, :], in_=f_planes[piece][:, :, COLS_HALF:].rearrange("p j c -> p c j")
+        def tanh_of_differences(piece):
+            n_bias = of_piece(piece)[3]
+            nc.scalar.activation(
+                out=f_grouped[piece][:, n_bias * V - cols_gp(piece) :, :],
+                in_=diffs[piece][:].rearrange("p j c -> p c j"),
+                func=ACT.Tanh,
             )
 
+        def regroup_gp(piece):
+            if cols_gp(piece):
+                f_grouped_gp[piece] = gp_pool.tile([P, COLS_GP, PACK], BF16, name="f_grouped_gp", align_bytes=64)
+                src = f_planes[piece][:, :, :COLS_GP].rearrange("p j c -> p c j")
+                if piece < PIECES_HEAD:
+                    nc.vector.tensor_copy(out=f_grouped_gp[piece][:], in_=src)
+                else:
+                    nc.gpsimd.tensor_scalar(
+                        out=f_grouped_gp[piece][:], in0=src, scalar1=1.0, scalar2=0.0, op0=ALU.mult, op1=ALU.add
+                    )
+
+        def regroup(piece):
+            if piece < PIECES_HEAD:
+                regroup_gp(piece)
+            src = f_planes[piece][:, :, cols_gp(piece) :].rearrange("p j c -> p c j")
+            nc.vector.tensor_copy(out=f_grouped[piece][:, : src.shape[1], :], in_=src)
+
         def quantise(piece):
-            f_codes[piece] = code_pool.tile([P, CHUNK], U32, name="f_codes", align_bytes=64)
-            f_scales[piece] = code_pool.tile([P, CHUNK], U8, name="f_scales", align_bytes=64)
-            for src, cols in ((f_grouped_gp, slice(0, COLS_HALF)), (f_grouped, slice(COLS_HALF, CHUNK))):
+            n_cols = of_piece(piece)[2] * V
+            f_codes[piece] = code_pool.tile([P, n_cols], U32, name="f_codes", align_bytes=64)
+            f_scales[piece] = code_pool.tile([P, n_cols], U8, name="f_scales", align_bytes=64)
+            parts = [(f_grouped[piece], slice(cols_gp(piece), n_cols))]
+            if cols_gp(piece):
+                parts = [(f_grouped_gp[piece], slice(0, COLS_GP))] + parts
+            for src, cols in parts:
                 nc.vector.quantize_mx(
                     out=f_codes[piece][:, cols].bitcast(FP8X4),
                     scales=f_scales[piece][:, cols],
-                    in_=src[piece][:].rearrange("p c j -> p (c j)"),
+                    in_=src[:].rearrange("p c j -> p (c j)"),
                 )
-            if PIECES_BIAS <= piece + 1 < PIECES:
+            if PIECES_HEAD <= piece + 1 < PIECES:
                 regroup_gp(piece + 1)
 
         def multiply(tile_no):
             chunk, i = divmod(tile_no, N_TILES)
             n_cols = slice(P * i, P * (i + 1))
-            g_t[tile_no] = banks.tile([P, CHUNK], F32, name="g_t", tag="bank")
+            g_t[tile_no] = banks.tile([P, CHUNKS[chunk][2] * V], F32, name="g_t", tag="bank")
             for g in range(GROUPS):
                 nc.tensor.matmul_mx(
                     out=g_t[tile_no][:],
@@ -331,59 +354,73 @@ def tile_attgcn_pa_kernel(
 
         def finish(tile_no):
             chunk, i = divmod(tile_no, N_TILES)
-            b = chunk * U_CHUNK // V
-            u_in_b = chunk * U_CHUNK % V
-            result = out_pool.tile([P, CHUNK], F32, name="result")
+            b, first_u, n_u = CHUNKS[chunk]
+            result = out_pool.tile([P, n_u * V], F32, name="result")
             nc.vector.scalar_tensor_tensor(
                 out=result[:],
                 in0=g_t[tile_no][:],
                 scalar=lam_f[:, 0:1],
-                in1=a_plus[:, i, u_in_b * V : u_in_b * V + CHUNK],
+                in1=a_plus[:, i, first_u * V : (first_u + n_u) * V],
                 op0=ALU.mult,
                 op1=ALU.add,
             )
             nc.sync.dma_start(
-                out=out[b, P * i : P * (i + 1), u_in_b : u_in_b + U_CHUNK, :].rearrange("n u v -> n (u v)"),
+                out=out[b, P * i : P * (i + 1), first_u : first_u + n_u, :].rearrange("n u v -> n (u v)"),
                 in_=result[:],
             )
 
+        sort_second_half = (
+            lambda: sort_words(phi_sorted, phi_words, 1),
+            lambda: sort_words(theta_sorted, theta_words, 1),
+            lambda: sort_planes(1),
+        )
         for j in range(PACK):
             sum_over_t(0, j)
-        transpose_rows(0, 0)
-        tanh_piece(0)
+            if j < len(sort_second_half):
+                sort_second_half[j]()
+            tanh_by_bias(0, j)
+            tanh_by_bias(2, j)
+        copy_rows(0, 0, transpose_rows(0, 0))
         sum_over_t(1, 0)
-        regroup_gp(0)
+        tanh_by_bias(1, 0)
         regroup(0)
-        quantise(0)
-        for j in range(1, PACK):
-            sum_over_t(1, j)
-        tanh_piece(1)
         subtract(2)
-        tanh_piece(2)
-        transpose_rows(1, 0)
-        regroup_gp(1)
+        sum_over_t(1, 1)
+        tanh_by_bias(1, 1)
+        tanh_of_differences(2)
+        quantise(0)
+        sum_over_t(1, 2)
+        tanh_by_bias(1, 2)
+        regroup(2)
+        sum_over_t(1, 3)
+        tanh_by_bias(1, 3)
+        quantise(2)
+        copy_rows(1, 0, transpose_rows(1, 0))
         regroup(1)
         quantise(1)
         subtract(3)
         multiply_four(1)
-        tanh_piece(3)
+        subtract(4)
+        for j in range(PACK):
+            tanh_by_bias(3, j)
+        tanh_of_differences(3)
 
         for piece in range(2, PIECES + 2):
+            if has_differences(piece + 3):
+                subtract(piece + 3)
             if piece + 2 < PIECES:
-                subtract(piece + 2)
-                tanh_piece(piece + 2)
-            tiles = range(TILES_A_STEP * (piece - 2), TILES_A_STEP * (piece - 1))
-            if piece < LEAD:
-                for tile_no in tiles:
-                    finish(tile_no)
+                for j in range(PACK):
+                    tanh_by_bias(piece + 2, j)
+            if has_differences(piece + 2):
+                tanh_of_differences(piece + 2)
+            if 2 < piece < PIECES:
                 regroup(piece)
-                transpose_rows(piece - 2, 1)
                 quantise(piece)
-            else:
-                if piece < PIECES:
-                    regroup(piece)
-                    quantise(piece)
-                for tile_no in tiles:
-                    finish(tile_no)
+            for tile_no in range(TILES_A_STEP * (piece - 2), TILES_A_STEP * (piece - 1)):
+                finish(tile_no)
+            if 4 <= piece < 4 + GROUPS:
+                copy_rows(piece - 4, 1, rows_t)
             if piece <= PIECES:
                 multiply_four(piece)
+            if 3 <= piece < 3 + GROUPS:
+                rows_t = transpose_rows(piece - 3, 1)

@@ -181,15 +181,21 @@ def tile_attgcn_pa_kernel(
                 sort_planes(0)
         sort_words(theta_sorted, theta_words, 0)
 
-        lam_f = keep.tile([P, 1], F32)
-        nc.vector.tensor_copy(out=lam_f[:], in_=lam_bf[:])
-        lam_kappa_b = keep.tile([P, N_TILES], F32)
-        nc.vector.tensor_scalar_mul(out=lam_kappa_b[:], in0=kappa_b_sb[:], scalar1=lam_f[:, 0:1])
         bias_diff = keep.tile([P, GROUPS, PACK], F32)
         nc.vector.tensor_sub(out=bias_diff[:], in0=phi_b_sb[:], in1=theta_b_sb[:])
         a_plus = keep.tile([P, N_TILES, V * V], F32)
 
-        def prepare_a(i):
+        lam_f = keep.tile([P, 1], F32)
+        lam_kappa_b = keep.tile([P, N_TILES], F32)
+
+        def prepare_a(tiles):
+            if tiles.start == 0:
+                nc.vector.tensor_copy(out=lam_f[:], in_=lam_bf[:])
+            nc.vector.tensor_scalar_mul(out=lam_kappa_b[:, tiles], in0=kappa_b_sb[:, tiles], scalar1=lam_f[:, 0:1])
+            for i in range(tiles.start, tiles.stop):
+                prepare_a_tile(i)
+
+        def prepare_a_tile(i):
             nc.gpsimd.tensor_scalar(
                 out=a_plus[:, i, :],
                 in0=a_bf[:, i, :],
@@ -198,9 +204,6 @@ def tile_attgcn_pa_kernel(
                 op0=ALU.mult,
                 op1=ALU.add,
             )
-
-        for i in range(N_TILES):
-            prepare_a(i)
 
         p_th = keep.tile([P, GROUPS, PACK, B, 2, V], F32)
         rows = keep.tile([P, GROUPS, 2, PACK, P], F32)
@@ -369,15 +372,13 @@ def tile_attgcn_pa_kernel(
                 in_=result[:],
             )
 
-        sort_second_half = (
-            lambda: sort_words(phi_sorted, phi_words, 1),
-            lambda: sort_words(theta_sorted, theta_words, 1),
-            lambda: sort_planes(1),
-        )
+        sort_words(phi_sorted, phi_words, 1)
+        sort_words(theta_sorted, theta_words, 1)
+        sort_planes(1)
         for j in range(PACK):
             sum_over_t(0, j)
-            if j < len(sort_second_half):
-                sort_second_half[j]()
+            if j == 1:
+                prepare_a(slice(0, N_TILES // 2))
             tanh_by_bias(0, j)
             tanh_by_bias(2, j)
         copy_rows(0, 0, transpose_rows(0, 0))
@@ -398,6 +399,7 @@ def tile_attgcn_pa_kernel(
         copy_rows(1, 0, transpose_rows(1, 0))
         regroup(1)
         quantise(1)
+        prepare_a(slice(N_TILES // 2, N_TILES))
         subtract(3)
         multiply_four(1)
         subtract(4)

@@ -22,7 +22,6 @@ ROWS = B * V
 T_HALF = T // 2
 U_CHUNK = 16
 CHUNK = U_CHUNK * V
-COLS_GP = CHUNK // 2
 CHUNKS = [(b, u, U_CHUNK) for b in range(B) for u in range(0, V, U_CHUNK)][:-1] + [
     (B - 1, u, U_CHUNK // 2) for u in range(U_CHUNK, V, U_CHUNK // 2)
 ]
@@ -136,6 +135,14 @@ def tile_attgcn_pa_kernel(
         nc.vector.memset(warm[:], 0.0)
         nc.scalar.activation(out=warm[:, 1:2], in_=warm[:, 0:1], func=ACT.Tanh)
 
+        zeros = keep.tile([P, K_PASS], BF16)
+        nc.vector.memset(zeros[:], 0.0)
+
+        def warm_up(n):
+            for i in range(n):
+                scratch = banks.tile([P, K_PASS], F32, name="scratch", tag="bank")
+                nc.tensor.matmul(out=scratch[:], lhsT=zeros[:, :P], rhs=zeros[:], start=True, stop=True)
+
         x_words = x_sb[:].bitcast(F32)
         x_grouped = keep.tile([P, T, B, V, PACK], BF16, align_bytes=64)
         x_grouped_words = x_grouped[:].bitcast(F32)
@@ -167,7 +174,7 @@ def tile_attgcn_pa_kernel(
                 for b_low in range(2):
                     src = x_t[:, b_low].rearrange("p s (t v) -> p t v s", v=V)
                     dst = x_grouped_words[:, steps, 2 * pair + b_low, :, :]
-                    if pair == 0:
+                    if h == 0 and pair == 0:
                         nc.vector.tensor_copy(out=dst, in_=src)
                     else:
                         nc.scalar.copy(out=dst, in_=src)
@@ -180,6 +187,7 @@ def tile_attgcn_pa_kernel(
                 sort_words(phi_sorted, phi_words, 0)
                 sort_planes(0)
         sort_words(theta_sorted, theta_words, 0)
+        warm_up(3)
 
         bias_diff = keep.tile([P, GROUPS, PACK], F32)
         nc.vector.tensor_sub(out=bias_diff[:], in0=phi_b_sb[:], in1=theta_b_sb[:])
@@ -264,7 +272,7 @@ def tile_attgcn_pa_kernel(
             return piece < PIECES and of_piece(piece)[3] < of_piece(piece)[2]
 
         def cols_gp(piece):
-            return COLS_GP if of_piece(piece)[2] == U_CHUNK else 0
+            return of_piece(piece)[2] * V // 2
 
         def subtract(piece):
             b, first_u, n_u, n_bias, g = of_piece(piece)
@@ -304,15 +312,14 @@ def tile_attgcn_pa_kernel(
             )
 
         def regroup_gp(piece):
-            if cols_gp(piece):
-                f_grouped_gp[piece] = gp_pool.tile([P, COLS_GP, PACK], BF16, name="f_grouped_gp", align_bytes=64)
-                src = f_planes[piece][:, :, :COLS_GP].rearrange("p j c -> p c j")
-                if piece < PIECES_HEAD:
-                    nc.vector.tensor_copy(out=f_grouped_gp[piece][:], in_=src)
-                else:
-                    nc.gpsimd.tensor_scalar(
-                        out=f_grouped_gp[piece][:], in0=src, scalar1=1.0, scalar2=0.0, op0=ALU.mult, op1=ALU.add
-                    )
+            f_grouped_gp[piece] = gp_pool.tile([P, cols_gp(piece), PACK], BF16, name="f_grouped_gp", align_bytes=64)
+            src = f_planes[piece][:, :, : cols_gp(piece)].rearrange("p j c -> p c j")
+            if piece < PIECES_HEAD:
+                nc.vector.tensor_copy(out=f_grouped_gp[piece][:], in_=src)
+            else:
+                nc.gpsimd.tensor_scalar(
+                    out=f_grouped_gp[piece][:], in0=src, scalar1=1.0, scalar2=0.0, op0=ALU.mult, op1=ALU.add
+                )
 
         def regroup(piece):
             if piece < PIECES_HEAD:
@@ -321,13 +328,10 @@ def tile_attgcn_pa_kernel(
             nc.vector.tensor_copy(out=f_grouped[piece][:, : src.shape[1], :], in_=src)
 
         def quantise(piece):
-            n_cols = of_piece(piece)[2] * V
+            n_cols, n_gp = of_piece(piece)[2] * V, cols_gp(piece)
             f_codes[piece] = code_pool.tile([P, n_cols], U32, name="f_codes", align_bytes=64)
             f_scales[piece] = code_pool.tile([P, n_cols], U8, name="f_scales", align_bytes=64)
-            parts = [(f_grouped[piece], slice(cols_gp(piece), n_cols))]
-            if cols_gp(piece):
-                parts = [(f_grouped_gp[piece], slice(0, COLS_GP))] + parts
-            for src, cols in parts:
+            for src, cols in ((f_grouped_gp[piece], slice(0, n_gp)), (f_grouped[piece], slice(n_gp, n_cols))):
                 nc.vector.quantize_mx(
                     out=f_codes[piece][:, cols].bitcast(FP8X4),
                     scales=f_scales[piece][:, cols],
@@ -372,13 +376,15 @@ def tile_attgcn_pa_kernel(
                 in_=result[:],
             )
 
-        sort_words(phi_sorted, phi_words, 1)
-        sort_words(theta_sorted, theta_words, 1)
-        sort_planes(1)
+        sort_second_half = (
+            lambda: sort_words(phi_sorted, phi_words, 1),
+            lambda: sort_words(theta_sorted, theta_words, 1),
+            lambda: sort_planes(1),
+            lambda: prepare_a(slice(0, N_TILES // 2)),
+        )
         for j in range(PACK):
             sum_over_t(0, j)
-            if j == 1:
-                prepare_a(slice(0, N_TILES // 2))
+            sort_second_half[j]()
             tanh_by_bias(0, j)
             tanh_by_bias(2, j)
         copy_rows(0, 0, transpose_rows(0, 0))
@@ -408,8 +414,6 @@ def tile_attgcn_pa_kernel(
         tanh_of_differences(3)
 
         for piece in range(2, PIECES + 2):
-            if has_differences(piece + 3):
-                subtract(piece + 3)
             if piece + 2 < PIECES:
                 for j in range(PACK):
                     tanh_by_bias(piece + 2, j)
@@ -424,5 +428,7 @@ def tile_attgcn_pa_kernel(
                 copy_rows(piece - 4, 1, rows_t)
             if piece <= PIECES:
                 multiply_four(piece)
+            if has_differences(piece + 3):
+                subtract(piece + 3)
             if 3 <= piece < 3 + GROUPS:
                 rows_t = transpose_rows(piece - 3, 1)

from contextlib import ExitStack

import concourse.masks as masks
import concourse.mybir as mybir

F32 = mybir.dt.float32
BF16 = mybir.dt.bfloat16
I32 = mybir.dt.int32
U32 = mybir.dt.uint32
U8 = mybir.dt.uint8
FP8X4 = mybir.dt.float8_e4m3fn_x4
ALU = mybir.AluOpType
ACT = mybir.ActivationFunctionType

P = 128
PACK = 4
K_PASS = P * PACK
B, T, V, C, K = 4, 8, 32, 512, 1024
GROUPS = K // K_PASS
N_TILES = K // P
ROWS = B * V
T_HALF = T // 2
U_CHUNK = 16
CHUNK = U_CHUNK * V
CHUNKS = [(b, u, U_CHUNK) for b in range(B) for u in range(0, V, U_CHUNK)][:-1] + [
    (B - 1, u, U_CHUNK // 2) for u in range(U_CHUNK, V, U_CHUNK // 2)
]
PIECES = len(CHUNKS) * GROUPS
U_PE = 4
PIECES_BIAS = 2
PIECES_HEAD = 4
TILES_A_STEP = N_TILES // GROUPS

PHI_ROW, THETA_ROW, KAPPA_ROW = 0, 4, 0

FLOPS = 2 * (B * T * V) * C * (2 * K) + 2 * (B * V * V) * K * K


def tile_attgcn_pa_kernel(
    tc,
    x,
    A,
    lam,
    phi_w_words,
    phi_w_scales,
    phi_b,
    theta_w_words,
    theta_w_scales,
    theta_b,
    kappa_w_words,
    kappa_w_scales,
    kappa_b,
    out,
):
    nc = tc.nc
    with ExitStack() as ctx:
        ctx.enter_context(tc.manual_schedule())
        keep = ctx.enter_context(tc.tile_pool(name="keep", bufs=1))
        plane_pool = ctx.enter_context(tc.tile_pool(name="plane_pool", bufs=4))
        gp_pool = ctx.enter_context(tc.tile_pool(name="gp_pool", bufs=1))
        grouped_pool = ctx.enter_context(tc.tile_pool(name="grouped_pool", bufs=4))
        code_pool = ctx.enter_context(tc.tile_pool(name="code_pool", bufs=6))
        out_pool = ctx.enter_context(tc.tile_pool(name="out_pool", bufs=8))
        banks = ctx.enter_context(tc.psum_pool(name="banks", bufs=6))
        diff_banks = ctx.enter_context(tc.psum_pool(name="diff_banks", bufs=2))

        planes = keep.tile([P, K], U8, align_bytes=64)
        kappa_planes = keep.tile([P, K], U8, align_bytes=64)
        nc.vector.memset(planes[:].bitcast(I32), 0)
        nc.vector.memset(kappa_planes[:].bitcast(I32), 0)

        x_sb = keep.tile([P, 2, B, C], BF16)
        x_tiles = x.rearrange("b (h t) v c -> h (t v) b c", h=2)

        def load_scale_rows(tile, first_row, scales, quads=range(4)):
            groups = scales.shape[0]
            for quad in quads:
                first = 32 * quad + first_row
                nc.sync.dma_start(
                    out=tile[first : first + 4 * groups, :].bitcast(I32),
                    in_=scales[:, 4 * quad : 4 * quad + 4, :].bitcast(I32),
                )

        def load_words(words_sb, words):
            nc.sync.dma_start(out=words_sb.bitcast(I32), in_=words.rearrange("p n t -> p (n t)").bitcast(I32))

        phi_words = keep.tile([P, K], U32, align_bytes=64)
        theta_words = keep.tile([P, K], U32, align_bytes=64)
        first_half, second_half = slice(0, K_PASS), slice(K_PASS, K)
        nc.sync.dma_start(out=x_sb[:, 0], in_=x_tiles[0])
        load_scale_rows(planes, PHI_ROW, phi_w_scales, range(0, 3))
        nc.sync.dma_start(out=x_sb[:, 1], in_=x_tiles[1])
        load_words(phi_words[:, first_half], phi_w_words[0, :, first_half, :])
        load_scale_rows(planes, PHI_ROW, phi_w_scales, range(3, 4))
        load_words(theta_words[:, first_half], theta_w_words[0, :, first_half, :])
        load_scale_rows(planes, THETA_ROW, theta_w_scales)

        phi_b_sb = keep.tile([P, GROUPS, PACK], BF16)
        theta_b_sb = keep.tile([P, GROUPS, PACK], BF16)
        nc.sync.dma_start(out=phi_b_sb[:], in_=phi_b.rearrange("(g p j) -> p g j", p=P, j=PACK))
        nc.sync.dma_start(out=theta_b_sb[:], in_=theta_b.rearrange("(g p j) -> p g j", p=P, j=PACK))
        load_words(phi_words[:, second_half], phi_w_words[0, :, second_half, :])
        load_words(theta_words[:, second_half], theta_w_words[0, :, second_half, :])
        lam_bf = keep.tile([P, 1], BF16)
        nc.sync.dma_start(out=lam_bf[:], in_=lam.partition_broadcast(P))
        kappa_b_sb = keep.tile([P, N_TILES], BF16)
        with nc.allow_non_contiguous_dma(reason="1024 bias values, one to a partition and tile"):
            nc.sync.dma_start(out=kappa_b_sb[:], in_=kappa_b.rearrange("(i m) -> m i", m=P))

        a_bf = keep.tile([P, N_TILES, V * V], BF16)
        a_rows = A.rearrange("(i m) u v -> m i (u v)", m=P)
        for pair in range(N_TILES // 2):
            nc.sync.dma_start(out=a_bf[:, 2 * pair : 2 * pair + 2, :], in_=a_rows[:, 2 * pair : 2 * pair + 2, :])
        load_scale_rows(kappa_planes, KAPPA_ROW, kappa_w_scales)
        kappa_words = keep.tile([P, GROUPS, K], U32, align_bytes=64)
        for g in range(GROUPS):
            load_words(kappa_words[:, g, :], kappa_w_words[g])

        ident = keep.tile([P, P], F32)
        masks.make_identity(nc, ident[:])
        spread = {}
        for b_low in range(2):
            for u in range(U_CHUNK - U_PE, V, U_CHUNK):
                spread[b_low, u] = keep.tile([P, U_PE, V], F32, name="spread_%d_%d" % (b_low, u))
                row_p = 2 * V * b_low + u
                row_th = 2 * V * b_low + V
                nc.gpsimd.tensor_tensor(
                    out=spread[b_low, u][:],
                    in0=ident[:, row_p : row_p + U_PE].unsqueeze(2).to_broadcast([P, U_PE, V]),
                    in1=ident[:, row_th : row_th + V].unsqueeze(1).to_broadcast([P, U_PE, V]),
                    op=ALU.subtract,
                )

        warm = keep.tile([P, 2], F32)
        nc.vector.memset(warm[:], 0.0)
        nc.scalar.activation(out=warm[:, 1:2], in_=warm[:, 0:1], func=ACT.Tanh)

        zeros = keep.tile([P, K_PASS], BF16)
        nc.vector.memset(zeros[:], 0.0)

        def warm_up(n):
            for i in range(n):
                scratch = banks.tile([P, K_PASS], F32, name="scratch", tag="bank")
                nc.tensor.matmul(out=scratch[:], lhsT=zeros[:, :P], rhs=zeros[:], start=True, stop=True)

        x_words = x_sb[:].bitcast(F32)
        x_grouped = keep.tile([P, T, B, V, PACK], BF16, align_bytes=64)
        x_grouped_words = x_grouped[:].bitcast(F32)
        x_codes = keep.tile([P, T, ROWS], U32, align_bytes=64)
        x_scales = keep.tile([P, T, ROWS], U8, align_bytes=64)
        phi_sorted = keep.tile([P, GROUPS, PACK, P], U32, align_bytes=64)
        theta_sorted = keep.tile([P, GROUPS, PACK, P], U32, align_bytes=64)
        planes_sorted = keep.tile([P, GROUPS, PACK, P], U8, align_bytes=64)

        def sort_words(dst, src, g):
            nc.vector.tensor_copy(
                out=dst[:, g].bitcast(I32),
                in_=src[:, K_PASS * g : K_PASS * (g + 1)].bitcast(I32).rearrange("p (m j) -> p j m", j=PACK),
            )

        def sort_planes(g):
            nc.vector.tensor_copy(
                out=planes_sorted[:, g],
                in_=planes[:, K_PASS * g : K_PASS * (g + 1)].rearrange("p (m j) -> p j m", j=PACK),
            )

        for h in range(2):
            steps = slice(T_HALF * h, T_HALF * (h + 1))
            for pair in range(B // 2):
                x_t = banks.tile([P, 2, 2, P], F32, name="x_t", tag="bank")
                for b_low in range(2):
                    for s in range(2):
                        nc.tensor.transpose(x_t[:, b_low, s, :], x_words[:, h, 2 * pair + b_low, s : C // 2 : 2], ident[:])
                for b_low in range(2):
                    src = x_t[:, b_low].rearrange("p s (t v) -> p t v s", v=V)
                    dst = x_grouped_words[:, steps, 2 * pair + b_low, :, :]
                    if h == 0 and pair == 0:
                        nc.vector.tensor_copy(out=dst, in_=src)
                    else:
                        nc.scalar.copy(out=dst, in_=src)
            nc.vector.quantize_mx(
                out=x_codes[:, steps, :].rearrange("p t r -> p (t r)").bitcast(FP8X4),
                scales=x_scales[:, steps, :].rearrange("p t r -> p (t r)"),
                in_=x_grouped[:, steps].rearrange("p t b v j -> p (t b v j)"),
            )
            if h == 0:
                sort_words(phi_sorted, phi_words, 0)
                sort_planes(0)
        sort_words(theta_sorted, theta_words, 0)
        warm_up(3)

        bias_diff = keep.tile([P, GROUPS, PACK], F32)
        nc.vector.tensor_sub(out=bias_diff[:], in0=phi_b_sb[:], in1=theta_b_sb[:])
        a_plus = keep.tile([P, N_TILES, V * V], F32)

        lam_f = keep.tile([P, 1], F32)
        lam_kappa_b = keep.tile([P, N_TILES], F32)

        def prepare_a(tiles):
            if tiles.start == 0:
                nc.vector.tensor_copy(out=lam_f[:], in_=lam_bf[:])
            nc.vector.tensor_scalar_mul(out=lam_kappa_b[:, tiles], in0=kappa_b_sb[:, tiles], scalar1=lam_f[:, 0:1])
            for i in range(tiles.start, tiles.stop):
                prepare_a_tile(i)

        def prepare_a_tile(i):
            nc.gpsimd.tensor_scalar(
                out=a_plus[:, i, :],
                in0=a_bf[:, i, :],
                scalar1=1.0,
                scalar2=lam_kappa_b[:, i : i + 1],
                op0=ALU.mult,
                op1=ALU.add,
            )

        p_th = keep.tile([P, GROUPS, PACK, B, 2, V], F32)
        rows = keep.tile([P, GROUPS, 2, PACK, P], F32)

        def transpose_rows(g, b_high):
            rows_t = banks.tile([P, PACK, P], F32, name="rows_t", tag="bank")
            for j in range(PACK):
                nc.tensor.transpose(
                    rows_t[:, j, :],
                    p_th[:, g, j, 2 * b_high : 2 * b_high + 2].rearrange("p b s v -> p (b s v)"),
                    ident[:],
                )
            return rows_t

        def copy_rows(g, b_high, rows_t):
            nc.vector.tensor_copy(out=rows[:, g, b_high], in_=rows_t[:])

        def sum_over_t(g, j):
            sums = banks.tile([P, 2, ROWS], F32, name="sums", tag="bank")
            for side, (words, first_row) in enumerate(((phi_sorted, PHI_ROW), (theta_sorted, THETA_ROW))):
                for t in range(T):
                    nc.tensor.matmul_mx(
                        out=sums[:, side, :],
                        lhsT=words[:, g, j, :].bitcast(FP8X4),
                        lhsT_scale=planes_sorted[first_row:P, g, j, :],
                        rhs=x_codes[:, t, :].bitcast(FP8X4),
                        rhs_scale=x_scales[:, t, :],
                        start=(t == 0),
                        stop=(t == T - 1),
                    )
            nc.vector.tensor_scalar(
                out=p_th[:, g, j, :, 0, :],
                in0=sums[:, 0, :].rearrange("p (b v) -> p b v", v=V),
                scalar1=1.0 / T,
                scalar2=bias_diff[:, g, j : j + 1],
                op0=ALU.mult,
                op1=ALU.add,
            )
            nc.vector.tensor_scalar_mul(
                out=p_th[:, g, j, :, 1, :], in0=sums[:, 1, :].rearrange("p (b v) -> p b v", v=V), scalar1=1.0 / T
            )

        f_planes = {}
        f_grouped = {}
        f_grouped_gp = {}
        diffs = {}
        f_codes = {}
        f_scales = {}
        g_t = {}

        def of_piece(piece):
            chunk, g = divmod(piece, GROUPS)
            b, first_u, n_u = CHUNKS[chunk]
            n_bias = n_u if piece < PIECES_BIAS or n_u < U_CHUNK else n_u - U_PE
            return b, first_u, n_u, n_bias, g

        def has_differences(piece):
            return piece < PIECES and of_piece(piece)[3] < of_piece(piece)[2]

        def cols_gp(piece):
            return of_piece(piece)[2] * V // 2

        def subtract(piece):
            b, first_u, n_u, n_bias, g = of_piece(piece)
            b_high, b_low = divmod(b, 2)
            diffs[piece] = diff_banks.tile([P, PACK, U_PE * V], F32, name="diffs")
            for j in range(PACK):
                nc.tensor.matmul(
                    out=diffs[piece][:, j, :],
                    lhsT=rows[:, g, b_high, j, :],
                    rhs=spread[b_low, first_u + n_bias][:].rearrange("p u v -> p (u v)"),
                    start=True,
                    stop=True,
                )

        def tanh_by_bias(piece, j):
            b, first_u, n_u, n_bias, g = of_piece(piece)
            if j == 0:
                f_planes[piece] = plane_pool.tile([P, PACK, n_bias * V], BF16, name="f_planes")
                f_grouped[piece] = grouped_pool.tile(
                    [P, n_u * V - cols_gp(piece), PACK], BF16, name="f_grouped", align_bytes=64
                )
            for u in range(n_bias):
                nc.scalar.activation(
                    out=f_planes[piece][:, j, V * u : V * (u + 1)],
                    in_=p_th[:, g, j, b, 1, :],
                    func=ACT.Tanh,
                    bias=p_th[:, g, j, b, 0, first_u + u : first_u + u + 1],
                    scale=-1.0,
                )

        def tanh_of_differences(piece):
            n_bias = of_piece(piece)[3]
            nc.scalar.activation(
                out=f_grouped[piece][:, n_bias * V - cols_gp(piece) :, :],
                in_=diffs[piece][:].rearrange("p j c -> p c j"),
                func=ACT.Tanh,
            )

        def regroup_gp(piece):
            f_grouped_gp[piece] = gp_pool.tile([P, cols_gp(piece), PACK], BF16, name="f_grouped_gp", align_bytes=64)
            src = f_planes[piece][:, :, : cols_gp(piece)].rearrange("p j c -> p c j")
            if piece < PIECES_HEAD:
                nc.vector.tensor_copy(out=f_grouped_gp[piece][:], in_=src)
            else:
                nc.gpsimd.tensor_scalar(
                    out=f_grouped_gp[piece][:], in0=src, scalar1=1.0, scalar2=0.0, op0=ALU.mult, op1=ALU.add
                )

        def regroup(piece):
            if piece < PIECES_HEAD:
                regroup_gp(piece)
            src = f_planes[piece][:, :, cols_gp(piece) :].rearrange("p j c -> p c j")
            nc.vector.tensor_copy(out=f_grouped[piece][:, : src.shape[1], :], in_=src)

        def quantise(piece):
            n_cols, n_gp = of_piece(piece)[2] * V, cols_gp(piece)
            f_codes[piece] = code_pool.tile([P, n_cols], U32, name="f_codes", align_bytes=64)
            f_scales[piece] = code_pool.tile([P, n_cols], U8, name="f_scales", align_bytes=64)
            for src, cols in ((f_grouped_gp[piece], slice(0, n_gp)), (f_grouped[piece], slice(n_gp, n_cols))):
                nc.vector.quantize_mx(
                    out=f_codes[piece][:, cols].bitcast(FP8X4),
                    scales=f_scales[piece][:, cols],
                    in_=src[:].rearrange("p c j -> p (c j)"),
                )
            if PIECES_HEAD <= piece + 1 < PIECES:
                regroup_gp(piece + 1)

        def multiply(tile_no):
            chunk, i = divmod(tile_no, N_TILES)
            n_cols = slice(P * i, P * (i + 1))
            g_t[tile_no] = banks.tile([P, CHUNKS[chunk][2] * V], F32, name="g_t", tag="bank")
            for g in range(GROUPS):
                nc.tensor.matmul_mx(
                    out=g_t[tile_no][:],
                    lhsT=kappa_words[:, g, n_cols].bitcast(FP8X4),
                    lhsT_scale=kappa_planes[KAPPA_ROW + 4 * g : P, n_cols],
                    rhs=f_codes[GROUPS * chunk + g][:].bitcast(FP8X4),
                    rhs_scale=f_scales[GROUPS * chunk + g][:],
                    start=(g == 0),
                    stop=(g == GROUPS - 1),
                )

        def multiply_four(step):
            for tile_no in range(TILES_A_STEP * (step - 1), TILES_A_STEP * step):
                multiply(tile_no)

        def finish(tile_no):
            chunk, i = divmod(tile_no, N_TILES)
            b, first_u, n_u = CHUNKS[chunk]
            result = out_pool.tile([P, n_u * V], F32, name="result")
            nc.vector.scalar_tensor_tensor(
                out=result[:],
                in0=g_t[tile_no][:],
                scalar=lam_f[:, 0:1],
                in1=a_plus[:, i, first_u * V : (first_u + n_u) * V],
                op0=ALU.mult,
                op1=ALU.add,
            )
            nc.sync.dma_start(
                out=out[b, P * i : P * (i + 1), first_u : first_u + n_u, :].rearrange("n u v -> n (u v)"),
                in_=result[:],
            )

        sort_second_half = (
            lambda: sort_words(phi_sorted, phi_words, 1),
            lambda: sort_words(theta_sorted, theta_words, 1),
            lambda: sort_planes(1),
            lambda: prepare_a(slice(0, N_TILES // 2)),
        )
        for j in range(PACK):
            sum_over_t(0, j)
            sort_second_half[j]()
            tanh_by_bias(0, j)
            tanh_by_bias(2, j)
        copy_rows(0, 0, transpose_rows(0, 0))
        sum_over_t(1, 0)
        tanh_by_bias(1, 0)
        regroup(0)
        subtract(2)
        sum_over_t(1, 1)
        tanh_by_bias(1, 1)
        tanh_of_differences(2)
        quantise(0)
        sum_over_t(1, 2)
        tanh_by_bias(1, 2)
        regroup(2)
        sum_over_t(1, 3)
        tanh_by_bias(1, 3)
        quantise(2)
        copy_rows(1, 0, transpose_rows(1, 0))
        regroup(1)
        quantise(1)
        prepare_a(slice(N_TILES // 2, N_TILES))
        subtract(3)
        multiply_four(1)
        subtract(4)
        for j in range(PACK):
            tanh_by_bias(3, j)
        tanh_of_differences(3)

        for piece in range(2, PIECES + 2):
            if piece + 2 < PIECES:
                for j in range(PACK):
                    tanh_by_bias(piece + 2, j)
            if has_differences(piece + 2):
                tanh_of_differences(piece + 2)
            if 2 < piece < PIECES:
                regroup(piece)
                quantise(piece)
            for tile_no in range(TILES_A_STEP * (piece - 2), TILES_A_STEP * (piece - 1)):
                finish(tile_no)
            if 4 <= piece < 4 + GROUPS:
                copy_rows(piece - 4, 1, rows_t)
            if piece <= PIECES:
                multiply_four(piece)
            if has_differences(piece + 3):
                subtract(piece + 3)
            if 3 <= piece < 3 + GROUPS:
                rows_t = transpose_rows(piece - 3, 1)
